import numpy as np
import ml_dtypes


def mxq(x, axis, fmt="e4m3"):
    dtype, down = {"e4m3": (ml_dtypes.float8_e4m3fn, 7), "e5m2": (ml_dtypes.float8_e5m2, 14)}[fmt]
    v = np.moveaxis(np.asarray(x, np.float32).astype(ml_dtypes.bfloat16).astype(np.float64), axis, -1)
    blocks = v.reshape(v.shape[:-1] + (-1, 32))
    amax = np.abs(blocks).max(-1, keepdims=True)
    byte = np.maximum(np.where(amax > 0, np.frexp(amax)[1] - 1 + 127, 0) - down, 1)
    scale = np.exp2(byte - 127.0)
    codes = (blocks / scale).astype(np.float32).astype(dtype).astype(np.float64)
    return np.moveaxis((codes * scale).reshape(v.shape), -1, axis)


WIDE = False


def mx_kscale(k):
    if not WIDE:
        return np.ones(k)
    levels = np.array([10, -10, 5, -5, 0])
    a = np.random.permutation(np.resize(levels, k // 512 * 4)).reshape(k // 512, 4)
    idx = np.arange(k)
    return np.exp2(a[idx // 512, idx % 128 // 32])


BF16 = ml_dtypes.bfloat16


def bf(x):
    return np.asarray(x, np.float32).astype(BF16)


def f64(x):
    return np.asarray(x).astype(np.float64)


B, T, C = 4, 256, 1024
EPS = 1e-8


def sigmoid(z):
    return 1.0 / (1.0 + np.exp(-z))


def setup_inputs():
    s = mx_kscale(C)
    t = mx_kscale(C)
    g = 1.0 / np.sqrt(C)
    return {
        "x": bf(np.random.standard_normal((B, T, C)) * s),
        "a0": bf(np.random.standard_normal((B, C)) * t),
        "b0": bf(0.5 + np.random.uniform(size=(B, C))),
        "x_prev0": bf(np.random.standard_normal((B, C)) * s),
        "w": bf((0.5 + 2.0 * np.random.uniform(size=C)) / T),
        "u": bf(np.random.standard_normal(C) * 0.5),
        "mu_r": bf(np.random.uniform(size=C)),
        "mu_k": bf(np.random.uniform(size=C)),
        "mu_v": bf(np.random.uniform(size=C)),
        "W_r": bf(np.random.standard_normal((C, C)) * g / s[None, :]),
        "W_k": bf(np.random.standard_normal((C, C)) * g / s[None, :]),
        "W_v": bf(np.random.standard_normal((C, C)) * g / s[None, :] * t[:, None]),
        "W_out": bf(np.random.standard_normal((C, C)) * 2.0 * g / t[None, :]),
    }


def reference(x, a0, b0, x_prev0, w, u, mu_r, mu_k, mu_v, W_r, W_k, W_v, W_out):
    x, a0, b0, x_prev0 = f64(x), f64(a0), f64(b0), f64(x_prev0)
    w, u = f64(w), f64(u)
    mu_r, mu_k, mu_v = f64(mu_r), f64(mu_k), f64(mu_v)
    x_shift = np.concatenate([x_prev0[:, None, :], x[:, :-1, :]], axis=1)
    xr = mu_r * x + (1.0 - mu_r) * x_shift
    xk = mu_k * x + (1.0 - mu_k) * x_shift
    xv = mu_v * x + (1.0 - mu_v) * x_shift
    r = sigmoid(mxq(xr, 2, "e4m3") @ mxq(f64(W_r), 1, "e4m3").T)
    k = mxq(xk, 2, "e4m3") @ mxq(f64(W_k), 1, "e4m3").T
    v = mxq(xv, 2, "e4m3") @ mxq(f64(W_v), 1, "e4m3").T
    ek = np.exp(u + k)
    steps = np.arange(1, T + 1).astype(np.float64)
    decay_pow = np.exp(-w[None, :] * steps[:, None])
    a_t = a0[:, None, :] * decay_pow[None]
    b_t = b0[:, None, :] * decay_pow[None]
    wkv = (a_t + ek * v) / (b_t + ek + EPS)
    h = r * wkv
    return mxq(h, 2, "e4m3") @ mxq(f64(W_out), 1, "e4m3").T

@@ -1,0 +1,451 @@
+import math
+from contextlib import ExitStack
+
+import concourse.mybir as mybir
+from concourse.masks import make_identity
+
+F32 = mybir.dt.float32
+BF16 = mybir.dt.bfloat16
+U32 = mybir.dt.uint32
+U8 = mybir.dt.uint8
+I32 = mybir.dt.int32
+FP8X4 = mybir.dt.float8_e4m3fn_x4
+ALU = mybir.AluOpType
+AF = mybir.ActivationFunctionType
+
+P = 128
+C = 1024
+NTOK = 1024
+T = 256
+HALF = 512
+EPS = 1e-8
+FLOPS = 4 * 2 * 1024 * 1024 * 1024
+PIN = True
+N_ACT_REGROUP = (2, 1, 2, 1)
+
+V_W, V_U, V_MUR, V_MUK, V_MUV, V_A0, V_B0 = 0, 1, 2, 3, 4, 5, 9
+
+
+def tile_rwkv_timemix_pa_kernel(
+    tc, x, a0, b0, x_prev0, w, u, mu_r, mu_k, mu_v, W_r, W_k, W_v, W_out, out
+):
+    nc = tc.nc
+    x_flat = x.flatten_outer_dims()
+    out_flat = out.flatten_outer_dims()
+    weights = (W_r, W_k, W_v, W_out)
+    with ExitStack() as ctx:
+        keep = ctx.enter_context(tc.tile_pool(name="keep", bufs=1))
+        gpool = ctx.enter_context(tc.tile_pool(name="gpool", bufs=2))
+        psum = ctx.enter_context(tc.psum_pool(name="psum", bufs=8))
+        if PIN:
+            ctx.enter_context(tc.manual_schedule())
+
+        def bank_tile(name):
+            return psum.tile([P, HALF], F32, tag="ps", name=name)
+
+        sm = keep.tile([P, 256], BF16)
+        nc.vector.memset(sm[:], 0.0)
+        epsT = keep.tile([P, 1], F32)
+        nc.vector.memset(epsT[:], EPS)
+        identF = keep.tile([P, P], F32)
+        make_identity(nc, identF[:])
+        identB = keep.tile([P, P], BF16)
+        make_identity(nc, identB[:])
+        negB = keep.tile([P, P], BF16)
+        nc.vector.tensor_scalar_mul(out=negB[:], in0=identB[:], scalar1=-1.0)
+        iota_i = keep.tile([P, T], I32)
+        nc.gpsimd.iota(iota_i[:], pattern=[[1, T]], base=1, channel_multiplier=0)
+        iota1 = keep.tile([P, T], F32)
+        nc.vector.tensor_copy(out=iota1[:], in_=iota_i[:])
+        smt = keep.tile([P, P], F32)
+        sc = keep.tile([P, 256], F32)
+        negw = keep.tile([P, 8], F32)
+        rb = keep.tile([P, 32], F32)
+        alpha = keep.tile([P, 32], F32)
+        gbias = keep.tile([P, 32], F32)
+
+        def scal(v, m):
+            return sc[:, 8 * v + m : 8 * v + m + 1]
+
+        wc = [keep.tile([P, 2, C], U32, align_bytes=64, name="wc%d" % i) for i in range(4)]
+        ws = [keep.tile([P, 2, C], U8, align_bytes=64, name="ws%d" % i) for i in range(4)]
+        xc = [keep.tile([P, 2, NTOK], U32, align_bytes=64, name="xc%d" % i) for i in range(3)]
+        xsc = [keep.tile([P, 2, NTOK], U8, align_bytes=64, name="xsc%d" % i) for i in range(3)]
+        hc = keep.tile([P, 2, NTOK], U32, align_bytes=64)
+        hs = keep.tile([P, 2, NTOK], U8, align_bytes=64)
+        q = keep.tile([P, 8, NTOK], F32)
+        gam = {}
+
+        def gamma(grp, part, parts):
+            h, g2 = grp // 2, grp % 2
+            if part == 0:
+                gam[grp] = gpool.tile([P, 4, HALF], F32, tag="gam", name="gam")
+            todo = [(j, bb) for j in range(4) for bb in range(2)]
+            n = len(todo) // parts
+            for j, bb in todo[part * n : part * n + n]:
+                m, b = 4 * g2 + j, 2 * h + bb
+                nc.scalar.activation(
+                    out=gam[grp][:, j, T * bb : T * bb + T],
+                    in_=iota1[:],
+                    func=AF.Sigmoid,
+                    scale=negw[:, m : m + 1],
+                    bias=gbias[:, 8 * b + m : 8 * b + m + 1],
+                )
+
+        def phase_a(pa):
+            xs_nat, x_nat, wnat, xsT, dbank, planes, wgt = {}, {}, {}, {}, {}, {}, {}
+
+            def load_x(h):
+                xs_t = pa.tile([P, 4, C], BF16, tag="xnat", bufs=4, name="xs_nat")
+                if h == 0:
+                    nc.sync.dma_start(out=xs_t[8:128, 0, :], in_=x_flat[7:127, :])
+                    nc.sync.dma_start(out=xs_t[1:8, 0, :], in_=x_flat[0:7, :])
+                    nc.sync.dma_start(
+                        out=xs_t[:, 1:4, :], in_=x_flat[127:511, :].rearrange("(i p) c -> p i c", p=P)
+                    )
+                else:
+                    nc.sync.dma_start(
+                        out=xs_t[:, :, :], in_=x_flat[511:1023, :].rearrange("(i p) c -> p i c", p=P)
+                    )
+                nc.sync.dma_start(
+                    out=xs_t[0:1, 0:4:2, :],
+                    in_=x_prev0[2 * h : 2 * h + 2, :].rearrange("(o b) c -> o b c", o=1),
+                )
+                x_t = pa.tile([P, 4, C], BF16, tag="xnat", bufs=4, name="x_nat")
+                nc.sync.dma_start(
+                    out=x_t[:, :, :],
+                    in_=x_flat[HALF * h : HALF * h + HALF, :].rearrange("(i p) c -> p i c", p=P),
+                )
+                xs_nat[h] = xs_t
+                x_nat[h] = x_t
+
+            def w_load(s):
+                wi, t4 = s // 4, s % 4
+                if wi < 3:
+                    view = weights[wi].rearrange("(g r e) c -> r g e c", r=P, e=2)
+                else:
+                    view = weights[wi].rearrange("(g e r) c -> r g e c", r=P, e=2)
+                wn = pa.tile([P, 2, C], BF16, tag="wnat", bufs=3, name="wnat")
+                nc.sync.dma_start(out=wn[:, :, :], in_=view[:, t4, :, :])
+                wnat[s] = wn
+
+            def w_transposes(s, g):
+                bank = bank_tile("ps_w")
+                for uu in range(2):
+                    for blk in range(2):
+                        col = (2 * uu + blk) * P
+                        nc.tensor.transpose(
+                            bank[:, col : col + P],
+                            wnat[s][:, blk, :].bitcast(F32)[:, 256 * g + P * uu : 256 * g + P * uu + P],
+                            identF[:],
+                        )
+                return bank
+
+            def w_evac(s, g, bank):
+                wg = pa.tile([P, HALF], F32, tag="wg", bufs=4, align_bytes=64, name="wg")
+                nc.scalar.copy(
+                    out=wg[:].rearrange("p (o u) -> p o u", u=2),
+                    in_=bank[:].rearrange("p (u o) -> p o u", u=2),
+                )
+                wgt[(s, g)] = wg
+
+            def w_quant(s, g):
+                wi, t4 = s // 4, s % 4
+                nc.vector.quantize_mx(
+                    out=wc[wi][:, g, 256 * t4 : 256 * t4 + 256].bitcast(FP8X4),
+                    scales=ws[wi][:, g, 256 * t4 : 256 * t4 + 256],
+                    in_=wgt[(s, g)][:].bitcast(BF16),
+                )
+
+            def xs_block(h, gu, on_act):
+                bank = bank_tile("ps_xs")
+                for i in range(4):
+                    nc.tensor.transpose(
+                        bank[:, P * i : P * i + P],
+                        xs_nat[h][:, i, :].bitcast(F32)[:, P * gu : P * gu + P],
+                        identF[:],
+                    )
+                t = pa.tile([P, HALF], F32, tag="xsT", bufs=5, name="xsT")
+                if on_act:
+                    nc.scalar.copy(out=t[:], in_=bank[:])
+                else:
+                    nc.vector.tensor_copy(out=t[:], in_=bank[:])
+                xsT[(h, gu)] = t
+
+            def d_plane(s):
+                h, m = s // 8, s % 8
+                gu, e = m // 2, m % 2
+                bank = bank_tile("ps_d")
+                lo, hi = 256 * gu + e, 256 * gu + 256
+                for i in range(4):
+                    nc.tensor.matmul(
+                        bank[:, P * i : P * i + P], lhsT=x_nat[h][:, i, lo:hi:2], rhs=identB[:],
+                        start=True, stop=False,
+                    )
+                    nc.tensor.matmul(
+                        bank[:, P * i : P * i + P], lhsT=xs_nat[h][:, i, lo:hi:2], rhs=negB[:],
+                        start=False, stop=True,
+                    )
+                dbank[s] = bank
+
+            def mix_plane(s):
+                h, m = s // 8, s % 8
+                gu, e, j, grp = m // 2, m % 2, m % 4, s // 4
+                if j == 0:
+                    planes[grp] = [
+                        pa.tile([P, 4, HALF], BF16, tag="planes", bufs=6, name="planes%d" % i) for i in range(3)
+                    ]
+                shifted = xsT[(h, gu)][:].bitcast(BF16).rearrange("p (t e) -> p t e", e=2)[:, :, e]
+                for mix in range(3):
+                    nc.vector.scalar_tensor_tensor(
+                        out=planes[grp][mix][:, j, :],
+                        in0=dbank[s][:],
+                        scalar=scal(V_MUR + mix, m),
+                        in1=shifted,
+                        op0=ALU.mult,
+                        op1=ALU.add,
+                    )
+
+            def regroup(grp, mix, on_act):
+                grouped = pa.tile([P, HALF, 4], BF16, tag="grouped", bufs=3, align_bytes=64, name="grouped")
+                dst = grouped[:].rearrange("p (c i) j -> p c j i", i=4)
+                src = planes[grp][mix][:].rearrange("p j (c i) -> p c j i", i=4)
+                if on_act:
+                    nc.scalar.copy(out=dst, in_=src)
+                else:
+                    nc.vector.tensor_copy(out=dst, in_=src)
+                return (grp, mix, grouped)
+
+            def x_quant(item):
+                grp, mix, grouped = item
+                h, g = grp // 2, grp % 2
+                tok = slice(HALF * h, HALF * h + HALF)
+                nc.vector.quantize_mx(
+                    out=xc[mix][:, g, tok].bitcast(FP8X4),
+                    scales=xsc[mix][:, g, tok],
+                    in_=grouped[:].rearrange("p t j -> p (t j)"),
+                )
+
+            def ln_table(n):
+                m, b = n // 4, n % 4
+                nc.scalar.activation(
+                    out=q[:, m, T * b : T * b + T], in_=dec[:, m, :], func=AF.Ln,
+                    scale=scal(V_B0 + b, m), bias=epsT[:],
+                )
+
+            for v, vec in ((V_W, w), (V_U, u), (V_MUR, mu_r), (V_MUK, mu_k), (V_MUV, mu_v)):
+                nc.scalar.dma_start(out=sm[4 * v : 4 * v + 4, :], in_=vec.rearrange("(r c) -> r c", c=256))
+            nc.scalar.dma_start(out=sm[4 * V_A0 : 4 * V_A0 + 16, :], in_=a0.rearrange("b (r c) -> (b r) c", c=256))
+            nc.scalar.dma_start(out=sm[4 * V_B0 : 4 * V_B0 + 16, :], in_=b0.rearrange("b (r c) -> (b r) c", c=256))
+            load_x(0)
+            for s in range(3):
+                w_load(s)
+            load_x(1)
+
+            ps_sm = bank_tile("ps_sm")
+            nc.tensor.transpose(ps_sm[:, 0:P], sm[:].bitcast(F32), identF[:])
+            nc.vector.tensor_copy(out=smt[:], in_=ps_sm[:, 0:P])
+            nc.vector.tensor_copy(out=sc[:], in_=smt[:].bitcast(BF16))
+            nc.vector.tensor_scalar_mul(out=negw[:], in0=sc[:, 8 * V_W : 8 * V_W + 8], scalar1=-1.0)
+            dec = gpool.tile([P, 8, T], F32, tag="gam", name="dec")
+            for m in range(8):
+                nc.scalar.activation(out=dec[:, m, :], in_=iota1[:], func=AF.Exp, scale=negw[:, m : m + 1])
+            nc.scalar.activation(out=gbias[:], in_=sc[:, 8 * V_B0 : 8 * V_B0 + 32], func=AF.Ln)
+            for gu in range(4):
+                xs_block(0, gu, False)
+            d_plane(0)
+            nc.vector.reciprocal(out=rb[:], in_=sc[:, 8 * V_B0 : 8 * V_B0 + 32])
+            nc.vector.tensor_tensor(out=alpha[:], in0=sc[:, 8 * V_A0 : 8 * V_A0 + 32], in1=rb[:], op=ALU.mult)
+            nc.vector.tensor_scalar_add(out=gbias[:], in0=gbias[:], scalar1=-math.log(EPS))
+
+            act_regroups = []
+            quants = {}
+            n_ln = 0
+            for s in range(16):
+                banks = [w_transposes(s, g) for g in range(2)]
+                if s + 3 < 16:
+                    w_load(s + 3)
+                if 3 <= s < 7:
+                    xs_block(1, s - 3, True)
+                if s + 1 < 16:
+                    d_plane(s + 1)
+                for g in range(2):
+                    w_evac(s, g, banks[g])
+                for k in range(3):
+                    if n_ln < 32:
+                        ln_table(n_ln)
+                        n_ln += 1
+                for grp, mix in act_regroups:
+                    quants[s + 1] = quants.get(s + 1, []) + [regroup(grp, mix, True)]
+                act_regroups = []
+                if s >= 12:
+                    gamma((s - 12) // 2, s % 2, 2)
+                mix_plane(s)
+                if s > 0:
+                    for g in range(2):
+                        w_quant(s - 1, g)
+                for item in quants.get(s, []):
+                    x_quant(item)
+                if s % 4 == 3:
+                    grp = s // 4
+                    n_act = N_ACT_REGROUP[grp]
+                    act_regroups = [(grp, mix) for mix in range(n_act)]
+                    for mix in range(n_act, 3):
+                        quants[s + 1] = quants.get(s + 1, []) + [regroup(grp, mix, False)]
+            for grp, mix in act_regroups:
+                quants[16] = quants.get(16, []) + [regroup(grp, mix, True)]
+            for g in range(2):
+                w_quant(15, g)
+            for item in quants.get(16, []):
+                x_quant(item)
+
+        def phase_b(pb):
+            acc, ys, wgrp, rgrp, ots = {}, {}, {}, {}, {}
+
+            def mx1(un):
+                h, m = un // 8, un % 8
+                tok = slice(HALF * h, HALF * h + HALF)
+                for wi in (1, 2, 0):
+                    ps = bank_tile("ps_s1")
+                    for g in range(2):
+                        nc.tensor.matmul_mx(
+                            out=ps[:],
+                            lhsT=wc[wi][:, g, P * m : P * m + P].bitcast(FP8X4),
+                            lhsT_scale=ws[wi][:, g, P * m : P * m + P],
+                            rhs=xc[wi][:, g, tok].bitcast(FP8X4),
+                            rhs_scale=xsc[wi][:, g, tok],
+                            start=(g == 0),
+                            stop=(g == 1),
+                        )
+                    acc[(un, wi)] = ps
+
+            def front(un):
+                h, m = un // 8, un % 8
+                j, grp = m % 4, un // 4
+                tok = slice(HALF * h, HALF * h + HALF)
+                if j == 0:
+                    wgrp[grp] = pb.tile([P, 4, HALF], F32, tag="grp", bufs=4, name="wgrp")
+                    rgrp[grp] = pb.tile([P, 4, HALF], F32, tag="grp", bufs=4, name="rgrp")
+                y_t = pb.tile([P, HALF], F32, tag="y", bufs=3, name="y_t")
+                ys[un] = y_t
+                nc.vector.tensor_tensor(out=y_t[:], in0=acc[(un, 1)][:], in1=q[:, m, tok], op=ALU.subtract)
+                nc.scalar.activation(out=y_t[:], in_=y_t[:], func=AF.Sigmoid, bias=scal(V_U, m))
+                nc.scalar.activation(out=rgrp[grp][:, j, :], in_=acc[(un, 0)][:], func=AF.Sigmoid)
+
+            def front2(un):
+                h, m = un // 8, un % 8
+                j, grp = m % 4, un // 4
+                for bb in range(2):
+                    b = 2 * h + bb
+                    cols = slice(T * bb, T * bb + T)
+                    nc.vector.scalar_tensor_tensor(
+                        out=wgrp[grp][:, j, cols],
+                        in0=gam[grp][:, j, cols],
+                        scalar=alpha[:, 8 * b + m : 8 * b + m + 1],
+                        in1=acc[(un, 2)][:, cols],
+                        op0=ALU.mult,
+                        op1=ALU.subtract,
+                    )
+
+            def back(un):
+                h, m = un // 8, un % 8
+                j, grp = m % 4, un // 4
+                nc.vector.tensor_tensor(
+                    out=wgrp[grp][:, j, :], in0=wgrp[grp][:, j, :], in1=ys[un][:], op=ALU.mult
+                )
+
+            def back2(un):
+                h, m = un // 8, un % 8
+                j, grp = m % 4, un // 4
+                for bb in range(2):
+                    b = 2 * h + bb
+                    cols = slice(T * bb, T * bb + T)
+                    nc.vector.scalar_tensor_tensor(
+                        out=wgrp[grp][:, j, cols],
+                        in0=gam[grp][:, j, cols],
+                        scalar=alpha[:, 8 * b + m : 8 * b + m + 1],
+                        in1=wgrp[grp][:, j, cols],
+                        op0=ALU.mult,
+                        op1=ALU.subtract,
+                    )
+
+            def gate(grp):
+                grouped = pb.tile([P, HALF, 4], BF16, tag="grouped", bufs=2, align_bytes=64, name="grouped")
+                nc.vector.tensor_tensor(
+                    out=grouped[:].rearrange("p (c i) j -> p c j i", i=4),
+                    in0=wgrp[grp][:].rearrange("p j (c i) -> p c j i", i=4),
+                    in1=rgrp[grp][:].rearrange("p j (c i) -> p c j i", i=4),
+                    op=ALU.mult,
+                )
+                return grouped
+
+            def h_quant(grp, grouped):
+                h, g2 = grp // 2, grp % 2
+                tok = slice(HALF * h, HALF * h + HALF)
+                nc.vector.quantize_mx(
+                    out=hc[:, g2, tok].bitcast(FP8X4),
+                    scales=hs[:, g2, tok],
+                    in_=grouped[:].rearrange("p t j -> p (t j)"),
+                )
+
+            def stage2(h, n, on_act):
+                tt, oh = n // 2, n % 2
+                t0 = HALF * h + P * tt
+                if n % 4 == 0:
+                    ots[h] = pb.tile([P, 2, C], F32, tag="ot", bufs=2, name="ot")
+                ps = bank_tile("ps_s2")
+                for g in range(2):
+                    nc.tensor.matmul_mx(
+                        out=ps[:],
+                        lhsT=hc[:, g, t0 : t0 + P].bitcast(FP8X4),
+                        lhsT_scale=hs[:, g, t0 : t0 + P],
+                        rhs=wc[3][:, g, HALF * oh : HALF * oh + HALF].bitcast(FP8X4),
+                        rhs_scale=ws[3][:, g, HALF * oh : HALF * oh + HALF],
+                        start=(g == 0),
+                        stop=(g == 1),
+                    )
+                dst = ots[h][:, tt % 2, HALF * oh : HALF * oh + HALF]
+                if on_act:
+                    nc.scalar.copy(out=dst, in_=ps[:])
+                else:
+                    nc.vector.tensor_copy(out=dst, in_=ps[:])
+                if oh == 1:
+                    nc.sync.dma_start(out=out_flat[t0 : t0 + P, :], in_=ots[h][:, tt % 2, :])
+
+            mx1(0)
+            front(0)
+            front2(0)
+            to_gate = None
+            to_quant = None
+            for un in range(16):
+                if un + 1 < 16:
+                    mx1(un + 1)
+                    front(un + 1)
+                if to_quant is not None:
+                    h_quant(to_quant[0], to_quant[1])
+                    to_quant = None
+                back(un)
+                if to_gate is not None:
+                    to_quant = (to_gate, gate(to_gate))
+                    to_gate = None
+                if un + 1 < 16:
+                    front2(un + 1)
+                if un in (4, 5):
+                    gamma(2, un - 4, 2)
+                if un in (8, 9):
+                    gamma(3, un - 8, 2)
+                if un >= 9:
+                    stage2(0, un - 9, True)
+                back2(un)
+                if un % 4 == 3:
+                    to_gate = un // 4
+            stage2(0, 7, True)
+            to_quant = (to_gate, gate(to_gate))
+            h_quant(to_quant[0], to_quant[1])
+            for n in range(8):
+                stage2(1, n, n % 2 == 0)
+
+        with tc.tile_pool(name="pa", bufs=2) as pool_a:
+            phase_a(pool_a)
+        with tc.tile_pool(name="pb", bufs=2) as pool_b:
+            phase_b(pool_b)

@@ -91,6 +91,14 @@ def tile_rwkv_timemix_pa_kernel(
                     scale=negw[:, m : m + 1],
                     bias=gbias[:, 8 * b + m : 8 * b + m + 1],
                 )
+                nc.gpsimd.tensor_scalar(
+                    out=gam[grp][:, j, T * bb : T * bb + T],
+                    in0=gam[grp][:, j, T * bb : T * bb + T],
+                    scalar1=alpha[:, 8 * b + m : 8 * b + m + 1],
+                    scalar2=0.0,
+                    op0=ALU.mult,
+                    op1=ALU.add,
+                )
 
         def phase_a(pa):
             xs_nat, x_nat, wnat, xsT, dbank, planes, wgt = {}, {}, {}, {}, {}, {}, {}
@@ -333,19 +341,10 @@ def tile_rwkv_timemix_pa_kernel(
                 nc.scalar.activation(out=rgrp[grp][:, j, :], in_=acc[(un, 0)][:], func=AF.Sigmoid)
 
             def front2(un):
-                h, m = un // 8, un % 8
-                j, grp = m % 4, un // 4
-                for bb in range(2):
-                    b = 2 * h + bb
-                    cols = slice(T * bb, T * bb + T)
-                    nc.vector.scalar_tensor_tensor(
-                        out=wgrp[grp][:, j, cols],
-                        in0=gam[grp][:, j, cols],
-                        scalar=alpha[:, 8 * b + m : 8 * b + m + 1],
-                        in1=acc[(un, 2)][:, cols],
-                        op0=ALU.mult,
-                        op1=ALU.subtract,
-                    )
+                j, grp = un % 4, un // 4
+                nc.vector.tensor_tensor(
+                    out=wgrp[grp][:, j, :], in0=gam[grp][:, j, :], in1=acc[(un, 2)][:], op=ALU.subtract
+                )
 
             def back(un):
                 h, m = un // 8, un % 8
@@ -355,19 +354,11 @@ def tile_rwkv_timemix_pa_kernel(
                 )
 
             def back2(un):
-                h, m = un // 8, un % 8
-                j, grp = m % 4, un // 4
-                for bb in range(2):
-                    b = 2 * h + bb
-                    cols = slice(T * bb, T * bb + T)
-                    nc.vector.scalar_tensor_tensor(
-                        out=wgrp[grp][:, j, cols],
-                        in0=gam[grp][:, j, cols],
-                        scalar=alpha[:, 8 * b + m : 8 * b + m + 1],
-                        in1=wgrp[grp][:, j, cols],
-                        op0=ALU.mult,
-                        op1=ALU.subtract,
-                    )
+                j, grp = un % 4, un // 4
+                engine = nc.vector if un == 15 else nc.gpsimd
+                engine.tensor_tensor(
+                    out=wgrp[grp][:, j, :], in0=gam[grp][:, j, :], in1=wgrp[grp][:, j, :], op=ALU.subtract
+                )
 
             def gate(grp):
                 grouped = pb.tile([P, HALF, 4], BF16, tag="grouped", bufs=2, align_bytes=64, name="grouped")
@@ -425,18 +416,18 @@ def tile_rwkv_timemix_pa_kernel(
                     h_quant(to_quant[0], to_quant[1])
                     to_quant = None
                 back(un)
+                back2(un)
+                if un + 1 < 16:
+                    front2(un + 1)
                 if to_gate is not None:
                     to_quant = (to_gate, gate(to_gate))
                     to_gate = None
-                if un + 1 < 16:
-                    front2(un + 1)
                 if un in (4, 5):
                     gamma(2, un - 4, 2)
                 if un in (8, 9):
                     gamma(3, un - 8, 2)
                 if un >= 9:
                     stage2(0, un - 9, True)
-                back2(un)
                 if un % 4 == 3:
                     to_gate = un // 4
             stage2(0, 7, True)

@@ -21,7 +21,7 @@ HALF = 512
 EPS = 1e-8
 FLOPS = 4 * 2 * 1024 * 1024 * 1024
 PIN = True
-N_ACT_REGROUP = (2, 1, 2, 1)
+N_ACT_REGROUP = (2, 2, 2, 1)
 
 V_W, V_U, V_MUR, V_MUK, V_MUV, V_A0, V_B0 = 0, 1, 2, 3, 4, 5, 9
 
@@ -91,79 +91,70 @@ def tile_rwkv_timemix_pa_kernel(
                     scale=negw[:, m : m + 1],
                     bias=gbias[:, 8 * b + m : 8 * b + m + 1],
                 )
-                nc.gpsimd.tensor_scalar(
-                    out=gam[grp][:, j, T * bb : T * bb + T],
-                    in0=gam[grp][:, j, T * bb : T * bb + T],
-                    scalar1=alpha[:, 8 * b + m : 8 * b + m + 1],
-                    scalar2=0.0,
-                    op0=ALU.mult,
-                    op1=ALU.add,
-                )
+
+        wnat, wgt, cur = {}, {}, {}
+
+        def w_load(s):
+            wi, t4 = s // 4, s % 4
+            if wi < 3:
+                view = weights[wi].rearrange("(g r e) c -> r g e c", r=P, e=2)
+            else:
+                view = weights[wi].rearrange("(g e r) c -> r g e c", r=P, e=2)
+            wn = cur["pool"].tile([P, 2, C], BF16, tag="wnat", bufs=3, name="wnat")
+            nc.sync.dma_start(out=wn[:, :, :], in_=view[:, t4, :, :])
+            wnat[s] = wn
+
+        def w_transposes(s, g):
+            bank = bank_tile("ps_w")
+            for uu in range(2):
+                for blk in range(2):
+                    col = (2 * uu + blk) * P
+                    nc.tensor.transpose(
+                        bank[:, col : col + P],
+                        wnat[s][:, blk, :].bitcast(F32)[:, 256 * g + P * uu : 256 * g + P * uu + P],
+                        identF[:],
+                    )
+            return bank
+
+        def w_evac(s, g, bank):
+            wg = cur["pool"].tile([P, HALF], F32, tag="wg", bufs=4, align_bytes=64, name="wg")
+            nc.scalar.copy(
+                out=wg[:].rearrange("p (o u) -> p o u", u=2),
+                in_=bank[:].rearrange("p (u o) -> p o u", u=2),
+            )
+            wgt[(s, g)] = wg
+
+        def w_quant(s, g):
+            wi, t4 = s // 4, s % 4
+            nc.vector.quantize_mx(
+                out=wc[wi][:, g, 256 * t4 : 256 * t4 + 256].bitcast(FP8X4),
+                scales=ws[wi][:, g, 256 * t4 : 256 * t4 + 256],
+                in_=wgt[(s, g)][:].bitcast(BF16),
+            )
 
         def phase_a(pa):
-            xs_nat, x_nat, wnat, xsT, dbank, planes, wgt = {}, {}, {}, {}, {}, {}, {}
+            cur["pool"] = pa
+            xs_nat, x_nat, xsT, dbank, planes = {}, {}, {}, {}, {}
 
-            def load_x(h):
+            def load_x(h, pieces):
                 xs_t = pa.tile([P, 4, C], BF16, tag="xnat", bufs=4, name="xs_nat")
-                if h == 0:
-                    nc.sync.dma_start(out=xs_t[8:128, 0, :], in_=x_flat[7:127, :])
-                    nc.sync.dma_start(out=xs_t[1:8, 0, :], in_=x_flat[0:7, :])
-                    nc.sync.dma_start(
-                        out=xs_t[:, 1:4, :], in_=x_flat[127:511, :].rearrange("(i p) c -> p i c", p=P)
-                    )
-                else:
-                    nc.sync.dma_start(
-                        out=xs_t[:, :, :], in_=x_flat[511:1023, :].rearrange("(i p) c -> p i c", p=P)
-                    )
-                nc.sync.dma_start(
-                    out=xs_t[0:1, 0:4:2, :],
-                    in_=x_prev0[2 * h : 2 * h + 2, :].rearrange("(o b) c -> o b c", o=1),
-                )
                 x_t = pa.tile([P, 4, C], BF16, tag="xnat", bufs=4, name="x_nat")
-                nc.sync.dma_start(
-                    out=x_t[:, :, :],
-                    in_=x_flat[HALF * h : HALF * h + HALF, :].rearrange("(i p) c -> p i c", p=P),
-                )
                 xs_nat[h] = xs_t
                 x_nat[h] = x_t
-
-            def w_load(s):
-                wi, t4 = s // 4, s % 4
-                if wi < 3:
-                    view = weights[wi].rearrange("(g r e) c -> r g e c", r=P, e=2)
-                else:
-                    view = weights[wi].rearrange("(g e r) c -> r g e c", r=P, e=2)
-                wn = pa.tile([P, 2, C], BF16, tag="wnat", bufs=3, name="wnat")
-                nc.sync.dma_start(out=wn[:, :, :], in_=view[:, t4, :, :])
-                wnat[s] = wn
-
-            def w_transposes(s, g):
-                bank = bank_tile("ps_w")
-                for uu in range(2):
-                    for blk in range(2):
-                        col = (2 * uu + blk) * P
-                        nc.tensor.transpose(
-                            bank[:, col : col + P],
-                            wnat[s][:, blk, :].bitcast(F32)[:, 256 * g + P * uu : 256 * g + P * uu + P],
-                            identF[:],
+                rows = x_flat[HALF * h : HALF * h + HALF, :]
+                by_batch = rows.rearrange("(k p) c -> p k c", p=T)
+                width = C // pieces
+                for n in range(pieces):
+                    cs = slice(width * n, width * n + width)
+                    nc.sync.dma_start(out=xs_t[8:128, 0:4:2, cs], in_=by_batch[7:127, :, cs])
+                    nc.sync.dma_start(out=xs_t[:, 1:4:2, cs], in_=by_batch[127:255, :, cs])
+                    nc.sync.dma_start(out=x_t[:, :, cs], in_=rows[:, cs].rearrange("(i p) c -> p i c", p=P))
+                    if n == 0:
+                        nc.sync.dma_start(out=xs_t[1:8, 0:4:2, :], in_=by_batch[0:7, :, :])
+                        nc.sync.dma_start(
+                            out=xs_t[0:1, 0:4:2, :],
+                            in_=x_prev0[2 * h : 2 * h + 2, :].rearrange("(o b) c -> o b c", o=1),
                         )
-                return bank
-
-            def w_evac(s, g, bank):
-                wg = pa.tile([P, HALF], F32, tag="wg", bufs=4, align_bytes=64, name="wg")
-                nc.scalar.copy(
-                    out=wg[:].rearrange("p (o u) -> p o u", u=2),
-                    in_=bank[:].rearrange("p (u o) -> p o u", u=2),
-                )
-                wgt[(s, g)] = wg
-
-            def w_quant(s, g):
-                wi, t4 = s // 4, s % 4
-                nc.vector.quantize_mx(
-                    out=wc[wi][:, g, 256 * t4 : 256 * t4 + 256].bitcast(FP8X4),
-                    scales=ws[wi][:, g, 256 * t4 : 256 * t4 + 256],
-                    in_=wgt[(s, g)][:].bitcast(BF16),
-                )
 
             def xs_block(h, gu, on_act):
                 bank = bank_tile("ps_xs")
@@ -245,10 +236,10 @@ def tile_rwkv_timemix_pa_kernel(
                 nc.scalar.dma_start(out=sm[4 * v : 4 * v + 4, :], in_=vec.rearrange("(r c) -> r c", c=256))
             nc.scalar.dma_start(out=sm[4 * V_A0 : 4 * V_A0 + 16, :], in_=a0.rearrange("b (r c) -> (b r) c", c=256))
             nc.scalar.dma_start(out=sm[4 * V_B0 : 4 * V_B0 + 16, :], in_=b0.rearrange("b (r c) -> (b r) c", c=256))
-            load_x(0)
+            load_x(0, 2)
             for s in range(3):
                 w_load(s)
-            load_x(1)
+            load_x(1, 1)
 
             ps_sm = bank_tile("ps_sm")
             nc.tensor.transpose(ps_sm[:, 0:P], sm[:].bitcast(F32), identF[:])
@@ -260,8 +251,9 @@ def tile_rwkv_timemix_pa_kernel(
                 nc.scalar.activation(out=dec[:, m, :], in_=iota1[:], func=AF.Exp, scale=negw[:, m : m + 1])
             nc.scalar.activation(out=gbias[:], in_=sc[:, 8 * V_B0 : 8 * V_B0 + 32], func=AF.Ln)
             for gu in range(4):
-                xs_block(0, gu, False)
+                xs_block(0, gu, gu > 0)
             d_plane(0)
+            d_plane(1)
             nc.vector.reciprocal(out=rb[:], in_=sc[:, 8 * V_B0 : 8 * V_B0 + 32])
             nc.vector.tensor_tensor(out=alpha[:], in0=sc[:, 8 * V_A0 : 8 * V_A0 + 32], in1=rb[:], op=ALU.mult)
             nc.vector.tensor_scalar_add(out=gbias[:], in0=gbias[:], scalar1=-math.log(EPS))
@@ -270,26 +262,27 @@ def tile_rwkv_timemix_pa_kernel(
             quants = {}
             n_ln = 0
             for s in range(16):
-                banks = [w_transposes(s, g) for g in range(2)]
-                if s + 3 < 16:
+                if s + 2 < 16:
+                    d_plane(s + 2)
+                banks = [w_transposes(s, g) for g in range(2)] if s < 12 else []
+                if s + 3 < 12:
                     w_load(s + 3)
                 if 3 <= s < 7:
                     xs_block(1, s - 3, True)
-                if s + 1 < 16:
-                    d_plane(s + 1)
-                for g in range(2):
+                for g in range(len(banks)):
                     w_evac(s, g, banks[g])
                 for k in range(3):
                     if n_ln < 32:
                         ln_table(n_ln)
                         n_ln += 1
-                for grp, mix in act_regroups:
+                if act_regroups:
+                    grp, mix = act_regroups[0]
+                    act_regroups = act_regroups[1:]
                     quants[s + 1] = quants.get(s + 1, []) + [regroup(grp, mix, True)]
-                act_regroups = []
-                if s >= 12:
-                    gamma((s - 12) // 2, s % 2, 2)
+                if s in (12, 13):
+                    gamma(0, s - 12, 2)
                 mix_plane(s)
-                if s > 0:
+                if 0 < s < 13:
                     for g in range(2):
                         w_quant(s - 1, g)
                 for item in quants.get(s, []):
@@ -302,12 +295,11 @@ def tile_rwkv_timemix_pa_kernel(
                         quants[s + 1] = quants.get(s + 1, []) + [regroup(grp, mix, False)]
             for grp, mix in act_regroups:
                 quants[16] = quants.get(16, []) + [regroup(grp, mix, True)]
-            for g in range(2):
-                w_quant(15, g)
             for item in quants.get(16, []):
                 x_quant(item)
 
         def phase_b(pb):
+            cur["pool"] = pb
             acc, ys, wgrp, rgrp, ots = {}, {}, {}, {}, {}
 
             def mx1(un):
@@ -341,10 +333,19 @@ def tile_rwkv_timemix_pa_kernel(
                 nc.scalar.activation(out=rgrp[grp][:, j, :], in_=acc[(un, 0)][:], func=AF.Sigmoid)
 
             def front2(un):
-                j, grp = un % 4, un // 4
-                nc.vector.tensor_tensor(
-                    out=wgrp[grp][:, j, :], in0=gam[grp][:, j, :], in1=acc[(un, 2)][:], op=ALU.subtract
-                )
+                h, m = un // 8, un % 8
+                j, grp = m % 4, un // 4
+                for bb in range(2):
+                    b = 2 * h + bb
+                    cols = slice(T * bb, T * bb + T)
+                    nc.vector.scalar_tensor_tensor(
+                        out=wgrp[grp][:, j, cols],
+                        in0=gam[grp][:, j, cols],
+                        scalar=alpha[:, 8 * b + m : 8 * b + m + 1],
+                        in1=acc[(un, 2)][:, cols],
+                        op0=ALU.mult,
+                        op1=ALU.subtract,
+                    )
 
             def back(un):
                 h, m = un // 8, un % 8
@@ -354,11 +355,19 @@ def tile_rwkv_timemix_pa_kernel(
                 )
 
             def back2(un):
-                j, grp = un % 4, un // 4
-                engine = nc.vector if un == 15 else nc.gpsimd
-                engine.tensor_tensor(
-                    out=wgrp[grp][:, j, :], in0=gam[grp][:, j, :], in1=wgrp[grp][:, j, :], op=ALU.subtract
-                )
+                h, m = un // 8, un % 8
+                j, grp = m % 4, un // 4
+                for bb in range(2):
+                    b = 2 * h + bb
+                    cols = slice(T * bb, T * bb + T)
+                    nc.vector.scalar_tensor_tensor(
+                        out=wgrp[grp][:, j, cols],
+                        in0=gam[grp][:, j, cols],
+                        scalar=alpha[:, 8 * b + m : 8 * b + m + 1],
+                        in1=wgrp[grp][:, j, cols],
+                        op0=ALU.mult,
+                        op1=ALU.subtract,
+                    )
 
             def gate(grp):
                 grouped = pb.tile([P, HALF, 4], BF16, tag="grouped", bufs=2, align_bytes=64, name="grouped")
@@ -403,6 +412,8 @@ def tile_rwkv_timemix_pa_kernel(
                 if oh == 1:
                     nc.sync.dma_start(out=out_flat[t0 : t0 + P, :], in_=ots[h][:, tt % 2, :])
 
+            for s in range(12, 15):
+                w_load(s)
             mx1(0)
             front(0)
             front2(0)
@@ -416,23 +427,50 @@ def tile_rwkv_timemix_pa_kernel(
                     h_quant(to_quant[0], to_quant[1])
                     to_quant = None
                 back(un)
-                back2(un)
-                if un + 1 < 16:
-                    front2(un + 1)
                 if to_gate is not None:
                     to_quant = (to_gate, gate(to_gate))
                     to_gate = None
+                if un + 1 < 16:
+                    front2(un + 1)
+                if un in (0, 1):
+                    gamma(1, un, 2)
+                if 1 <= un < 5:
+                    banks = [w_transposes(11 + un, g) for g in range(2)]
+                    if un == 1:
+                        w_load(15)
+                    for g in range(2):
+                        w_evac(11 + un, g, banks[g])
+                if 2 <= un < 6:
+                    for g in range(2):
+                        w_quant(10 + un, g)
                 if un in (4, 5):
                     gamma(2, un - 4, 2)
                 if un in (8, 9):
                     gamma(3, un - 8, 2)
                 if un >= 9:
                     stage2(0, un - 9, True)
+                back2(un)
                 if un % 4 == 3:
                     to_gate = un // 4
             stage2(0, 7, True)
-            to_quant = (to_gate, gate(to_gate))
-            h_quant(to_quant[0], to_quant[1])
+            last = []
+            for part in range(2):
+                cols = slice(T * part, T * part + T)
+                grouped = pb.tile([P, T, 4], BF16, tag="grouped", bufs=2, align_bytes=64, name="grouped")
+                nc.vector.tensor_tensor(
+                    out=grouped[:].rearrange("p (c i) j -> p c j i", i=4),
+                    in0=wgrp[3][:, :, cols].rearrange("p j (c i) -> p c j i", i=4),
+                    in1=rgrp[3][:, :, cols].rearrange("p j (c i) -> p c j i", i=4),
+                    op=ALU.mult,
+                )
+                last.append(grouped)
+            for part in range(2):
+                tok = slice(HALF + T * part, HALF + T * part + T)
+                nc.vector.quantize_mx(
+                    out=hc[:, 1, tok].bitcast(FP8X4),
+                    scales=hs[:, 1, tok],
+                    in_=last[part][:].rearrange("p t j -> p (t j)"),
+                )
             for n in range(8):
                 stage2(1, n, n % 2 == 0)
 

@@ -21,7 +21,7 @@ HALF = 512
 EPS = 1e-8
 FLOPS = 4 * 2 * 1024 * 1024 * 1024
 PIN = True
-N_ACT_REGROUP = (2, 2, 2, 1)
+N_ACT_REGROUP = (1, 1, 1, 1)
 
 V_W, V_U, V_MUR, V_MUK, V_MUV, V_A0, V_B0 = 0, 1, 2, 3, 4, 5, 9
 
@@ -67,8 +67,10 @@ def tile_rwkv_timemix_pa_kernel(
         def scal(v, m):
             return sc[:, 8 * v + m : 8 * v + m + 1]
 
-        wc = [keep.tile([P, 2, C], U32, align_bytes=64, name="wc%d" % i) for i in range(4)]
-        ws = [keep.tile([P, 2, C], U8, align_bytes=64, name="ws%d" % i) for i in range(4)]
+        wc = [keep.tile([P, 4, 2, T], U32, align_bytes=64, name="wc%d" % i) for i in range(3)]
+        ws = [keep.tile([P, 4, 2, T], U8, align_bytes=64, name="ws%d" % i) for i in range(3)]
+        woc = keep.tile([P, 2, C], U32, align_bytes=64)
+        wos = keep.tile([P, 2, C], U8, align_bytes=64)
         xc = [keep.tile([P, 2, NTOK], U32, align_bytes=64, name="xc%d" % i) for i in range(3)]
         xsc = [keep.tile([P, 2, NTOK], U8, align_bytes=64, name="xsc%d" % i) for i in range(3)]
         hc = keep.tile([P, 2, NTOK], U32, align_bytes=64)
@@ -117,19 +119,27 @@ def tile_rwkv_timemix_pa_kernel(
             return bank
 
         def w_evac(s, g, bank):
-            wg = cur["pool"].tile([P, HALF], F32, tag="wg", bufs=4, align_bytes=64, name="wg")
+            if g == 0:
+                wgt[s] = cur["pool"].tile([P, 2, HALF], F32, tag="wg", bufs=2, align_bytes=64, name="wg")
             nc.scalar.copy(
-                out=wg[:].rearrange("p (o u) -> p o u", u=2),
+                out=wgt[s][:, g, :].rearrange("p (o u) -> p o u", u=2),
                 in_=bank[:].rearrange("p (u o) -> p o u", u=2),
             )
-            wgt[(s, g)] = wg
 
-        def w_quant(s, g):
+        def w_quant(s):
             wi, t4 = s // 4, s % 4
+            if wi == 3:
+                for g in range(2):
+                    nc.vector.quantize_mx(
+                        out=woc[:, g, T * t4 : T * t4 + T].bitcast(FP8X4),
+                        scales=wos[:, g, T * t4 : T * t4 + T],
+                        in_=wgt[s][:, g, :].bitcast(BF16),
+                    )
+                return
             nc.vector.quantize_mx(
-                out=wc[wi][:, g, 256 * t4 : 256 * t4 + 256].bitcast(FP8X4),
-                scales=ws[wi][:, g, 256 * t4 : 256 * t4 + 256],
-                in_=wgt[(s, g)][:].bitcast(BF16),
+                out=wc[wi][:, t4, :, :].rearrange("p g o -> p (g o)").bitcast(FP8X4),
+                scales=ws[wi][:, t4, :, :].rearrange("p g o -> p (g o)"),
+                in_=wgt[s][:].rearrange("p g w -> p (g w)").bitcast(BF16),
             )
 
         def phase_a(pa):
@@ -251,7 +261,7 @@ def tile_rwkv_timemix_pa_kernel(
                 nc.scalar.activation(out=dec[:, m, :], in_=iota1[:], func=AF.Exp, scale=negw[:, m : m + 1])
             nc.scalar.activation(out=gbias[:], in_=sc[:, 8 * V_B0 : 8 * V_B0 + 32], func=AF.Ln)
             for gu in range(4):
-                xs_block(0, gu, gu > 0)
+                xs_block(0, gu, False)
             d_plane(0)
             d_plane(1)
             nc.vector.reciprocal(out=rb[:], in_=sc[:, 8 * V_B0 : 8 * V_B0 + 32])
@@ -279,12 +289,11 @@ def tile_rwkv_timemix_pa_kernel(
                     grp, mix = act_regroups[0]
                     act_regroups = act_regroups[1:]
                     quants[s + 1] = quants.get(s + 1, []) + [regroup(grp, mix, True)]
-                if s in (12, 13):
-                    gamma(0, s - 12, 2)
+                if s >= 12:
+                    gamma((s - 12) // 2, s % 2, 2)
                 mix_plane(s)
                 if 0 < s < 13:
-                    for g in range(2):
-                        w_quant(s - 1, g)
+                    w_quant(s - 1)
                 for item in quants.get(s, []):
                     x_quant(item)
                 if s % 4 == 3:
@@ -300,18 +309,25 @@ def tile_rwkv_timemix_pa_kernel(
 
         def phase_b(pb):
             cur["pool"] = pb
-            acc, ys, wgrp, rgrp, ots = {}, {}, {}, {}, {}
+            acc, ygrp, wgrp, rgrp, ots, held = {}, {}, {}, {}, {}, {}
+
+            def flat(t):
+                return t[:].rearrange("p j t -> p (j t)")
+
+            def runs(t, cols):
+                return t[:, :, cols].rearrange("p j (c i) -> p c j i", i=4)
 
             def mx1(un):
                 h, m = un // 8, un % 8
                 tok = slice(HALF * h, HALF * h + HALF)
+                mc = slice(P * (m % 2), P * (m % 2) + P)
                 for wi in (1, 2, 0):
                     ps = bank_tile("ps_s1")
                     for g in range(2):
                         nc.tensor.matmul_mx(
                             out=ps[:],
-                            lhsT=wc[wi][:, g, P * m : P * m + P].bitcast(FP8X4),
-                            lhsT_scale=ws[wi][:, g, P * m : P * m + P],
+                            lhsT=wc[wi][:, m // 2, g, mc].bitcast(FP8X4),
+                            lhsT_scale=ws[wi][:, m // 2, g, mc],
                             rhs=xc[wi][:, g, tok].bitcast(FP8X4),
                             rhs_scale=xsc[wi][:, g, tok],
                             start=(g == 0),
@@ -321,20 +337,16 @@ def tile_rwkv_timemix_pa_kernel(
 
             def front(un):
                 h, m = un // 8, un % 8
-                j, grp = m % 4, un // 4
+                j, grp = un % 4, un // 4
                 tok = slice(HALF * h, HALF * h + HALF)
                 if j == 0:
-                    wgrp[grp] = pb.tile([P, 4, HALF], F32, tag="grp", bufs=4, name="wgrp")
-                    rgrp[grp] = pb.tile([P, 4, HALF], F32, tag="grp", bufs=4, name="rgrp")
-                y_t = pb.tile([P, HALF], F32, tag="y", bufs=3, name="y_t")
-                ys[un] = y_t
-                nc.vector.tensor_tensor(out=y_t[:], in0=acc[(un, 1)][:], in1=q[:, m, tok], op=ALU.subtract)
-                nc.scalar.activation(out=y_t[:], in_=y_t[:], func=AF.Sigmoid, bias=scal(V_U, m))
+                    ygrp[grp] = pb.tile([P, 4, HALF], F32, tag="grp", bufs=6, name="ygrp")
+                    wgrp[grp] = pb.tile([P, 4, HALF], F32, tag="grp", bufs=6, name="wgrp")
+                    rgrp[grp] = pb.tile([P, 4, HALF], F32, tag="grp", bufs=6, name="rgrp")
+                y_t = ygrp[grp][:, j, :]
+                nc.vector.tensor_tensor(out=y_t, in0=acc[(un, 1)][:], in1=q[:, m, tok], op=ALU.subtract)
+                nc.scalar.activation(out=y_t, in_=y_t, func=AF.Sigmoid, bias=scal(V_U, m))
                 nc.scalar.activation(out=rgrp[grp][:, j, :], in_=acc[(un, 0)][:], func=AF.Sigmoid)
-
-            def front2(un):
-                h, m = un // 8, un % 8
-                j, grp = m % 4, un // 4
                 for bb in range(2):
                     b = 2 * h + bb
                     cols = slice(T * bb, T * bb + T)
@@ -347,63 +359,58 @@ def tile_rwkv_timemix_pa_kernel(
                         op1=ALU.subtract,
                     )
 
-            def back(un):
-                h, m = un // 8, un % 8
-                j, grp = m % 4, un // 4
-                nc.vector.tensor_tensor(
-                    out=wgrp[grp][:, j, :], in0=wgrp[grp][:, j, :], in1=ys[un][:], op=ALU.mult
-                )
-
-            def back2(un):
-                h, m = un // 8, un % 8
-                j, grp = m % 4, un // 4
-                for bb in range(2):
-                    b = 2 * h + bb
-                    cols = slice(T * bb, T * bb + T)
-                    nc.vector.scalar_tensor_tensor(
-                        out=wgrp[grp][:, j, cols],
-                        in0=gam[grp][:, j, cols],
-                        scalar=alpha[:, 8 * b + m : 8 * b + m + 1],
-                        in1=wgrp[grp][:, j, cols],
-                        op0=ALU.mult,
-                        op1=ALU.subtract,
+            def long_step(grp, k):
+                h, g2 = grp // 2, grp % 2
+                if k == 0:
+                    nc.vector.tensor_tensor(out=flat(wgrp[grp]), in0=flat(wgrp[grp]), in1=flat(ygrp[grp]), op=ALU.mult)
+                elif k == 1:
+                    for j in range(4):
+                        for bb in range(2):
+                            m, b = 4 * g2 + j, 2 * h + bb
+                            cols = slice(T * bb, T * bb + T)
+                            nc.vector.scalar_tensor_tensor(
+                                out=wgrp[grp][:, j, cols],
+                                in0=gam[grp][:, j, cols],
+                                scalar=alpha[:, 8 * b + m : 8 * b + m + 1],
+                                in1=wgrp[grp][:, j, cols],
+                                op0=ALU.mult,
+                                op1=ALU.subtract,
+                            )
+                elif k == 2:
+                    grouped = pb.tile([P, HALF, 4], BF16, tag="grouped", bufs=2, align_bytes=64, name="grouped")
+                    nc.vector.tensor_tensor(
+                        out=grouped[:].rearrange("p (c i) j -> p c j i", i=4),
+                        in0=runs(wgrp[grp], slice(0, HALF)),
+                        in1=runs(rgrp[grp], slice(0, HALF)),
+                        op=ALU.mult,
+                    )
+                    held[grp] = grouped
+                else:
+                    tok = slice(HALF * h, HALF * h + HALF)
+                    nc.vector.quantize_mx(
+                        out=hc[:, g2, tok].bitcast(FP8X4),
+                        scales=hs[:, g2, tok],
+                        in_=held[grp][:].rearrange("p t j -> p (t j)"),
                     )
 
-            def gate(grp):
-                grouped = pb.tile([P, HALF, 4], BF16, tag="grouped", bufs=2, align_bytes=64, name="grouped")
-                nc.vector.tensor_tensor(
-                    out=grouped[:].rearrange("p (c i) j -> p c j i", i=4),
-                    in0=wgrp[grp][:].rearrange("p j (c i) -> p c j i", i=4),
-                    in1=rgrp[grp][:].rearrange("p j (c i) -> p c j i", i=4),
-                    op=ALU.mult,
-                )
-                return grouped
-
-            def h_quant(grp, grouped):
-                h, g2 = grp // 2, grp % 2
-                tok = slice(HALF * h, HALF * h + HALF)
-                nc.vector.quantize_mx(
-                    out=hc[:, g2, tok].bitcast(FP8X4),
-                    scales=hs[:, g2, tok],
-                    in_=grouped[:].rearrange("p t j -> p (t j)"),
+            def stage2_pass(h, n, g, ps):
+                tt, oh = n // 2, n % 2
+                t0 = HALF * h + P * tt
+                nc.tensor.matmul_mx(
+                    out=ps[:],
+                    lhsT=hc[:, g, t0 : t0 + P].bitcast(FP8X4),
+                    lhsT_scale=hs[:, g, t0 : t0 + P],
+                    rhs=woc[:, g, HALF * oh : HALF * oh + HALF].bitcast(FP8X4),
+                    rhs_scale=wos[:, g, HALF * oh : HALF * oh + HALF],
+                    start=(g == 0),
+                    stop=(g == 1),
                 )
 
-            def stage2(h, n, on_act):
+            def stage2_out(h, n, ps, on_act):
                 tt, oh = n // 2, n % 2
                 t0 = HALF * h + P * tt
                 if n % 4 == 0:
                     ots[h] = pb.tile([P, 2, C], F32, tag="ot", bufs=2, name="ot")
-                ps = bank_tile("ps_s2")
-                for g in range(2):
-                    nc.tensor.matmul_mx(
-                        out=ps[:],
-                        lhsT=hc[:, g, t0 : t0 + P].bitcast(FP8X4),
-                        lhsT_scale=hs[:, g, t0 : t0 + P],
-                        rhs=wc[3][:, g, HALF * oh : HALF * oh + HALF].bitcast(FP8X4),
-                        rhs_scale=ws[3][:, g, HALF * oh : HALF * oh + HALF],
-                        start=(g == 0),
-                        stop=(g == 1),
-                    )
                 dst = ots[h][:, tt % 2, HALF * oh : HALF * oh + HALF]
                 if on_act:
                     nc.scalar.copy(out=dst, in_=ps[:])
@@ -414,53 +421,47 @@ def tile_rwkv_timemix_pa_kernel(
 
             for s in range(12, 15):
                 w_load(s)
-            mx1(0)
-            front(0)
-            front2(0)
-            to_gate = None
-            to_quant = None
-            for un in range(16):
-                if un + 1 < 16:
-                    mx1(un + 1)
-                    front(un + 1)
-                if to_quant is not None:
-                    h_quant(to_quant[0], to_quant[1])
-                    to_quant = None
-                back(un)
-                if to_gate is not None:
-                    to_quant = (to_gate, gate(to_gate))
-                    to_gate = None
-                if un + 1 < 16:
-                    front2(un + 1)
-                if un in (0, 1):
-                    gamma(1, un, 2)
-                if 1 <= un < 5:
-                    banks = [w_transposes(11 + un, g) for g in range(2)]
-                    if un == 1:
-                        w_load(15)
-                    for g in range(2):
-                        w_evac(11 + un, g, banks[g])
-                if 2 <= un < 6:
-                    for g in range(2):
-                        w_quant(10 + un, g)
-                if un in (4, 5):
-                    gamma(2, un - 4, 2)
-                if un in (8, 9):
-                    gamma(3, un - 8, 2)
-                if un >= 9:
-                    stage2(0, un - 9, True)
-                back2(un)
-                if un % 4 == 3:
-                    to_gate = un // 4
-            stage2(0, 7, True)
+            for un in range(4):
+                mx1(un)
+                front(un)
+            open_banks = []
+            for grp in range(4):
+                for k in range(4):
+                    if grp < 3:
+                        mx1(4 * grp + 4 + k)
+                        front(4 * grp + 4 + k)
+                    if grp < 3 or k < 2:
+                        long_step(grp, k)
+                    if grp == 0:
+                        banks = [w_transposes(12 + k, g) for g in range(2)]
+                        if k == 0:
+                            w_load(15)
+                        for g in range(2):
+                            w_evac(12 + k, g, banks[g])
+                        if k > 0:
+                            w_quant(11 + k)
+                    if grp == 1 and k == 0:
+                        w_quant(15)
+                    if grp < 2 and k >= 2:
+                        gamma(grp + 2, k - 2, 2)
+                    if grp == 2:
+                        for n in (2 * k, 2 * k + 1):
+                            ps = bank_tile("ps_s2")
+                            stage2_pass(0, n, 0, ps)
+                            stage2_pass(0, n, 1, ps)
+                            stage2_out(0, n, ps, True)
+                    if grp == 3 and k == 0:
+                        for n in range(8):
+                            open_banks.append(bank_tile("ps_s2"))
+                            stage2_pass(1, n, 0, open_banks[n])
             last = []
             for part in range(2):
                 cols = slice(T * part, T * part + T)
                 grouped = pb.tile([P, T, 4], BF16, tag="grouped", bufs=2, align_bytes=64, name="grouped")
                 nc.vector.tensor_tensor(
                     out=grouped[:].rearrange("p (c i) j -> p c j i", i=4),
-                    in0=wgrp[3][:, :, cols].rearrange("p j (c i) -> p c j i", i=4),
-                    in1=rgrp[3][:, :, cols].rearrange("p j (c i) -> p c j i", i=4),
+                    in0=runs(wgrp[3], cols),
+                    in1=runs(rgrp[3], cols),
                     op=ALU.mult,
                 )
                 last.append(grouped)
@@ -472,7 +473,8 @@ def tile_rwkv_timemix_pa_kernel(
                     in_=last[part][:].rearrange("p t j -> p (t j)"),
                 )
             for n in range(8):
-                stage2(1, n, n % 2 == 0)
+                stage2_pass(1, n, 1, open_banks[n])
+                stage2_out(1, n, open_banks[n], n % 2 == 0)
 
         with tc.tile_pool(name="pa", bufs=2) as pool_a:
             phase_a(pool_a)

@@ -20,7 +20,7 @@ T = 256
 HALF = 512
 EPS = 1e-8
 FLOPS = 4 * 2 * 1024 * 1024 * 1024
-PIN = True
+PIN = False
 N_ACT_REGROUP = (1, 1, 1, 1)
 
 V_W, V_U, V_MUR, V_MUK, V_MUV, V_A0, V_B0 = 0, 1, 2, 3, 4, 5, 9

@@ -19,9 +19,7 @@ NTOK = 1024
 T = 256
 HALF = 512
 EPS = 1e-8
-FLOPS = 4 * 2 * 1024 * 1024 * 1024
-PIN = False
-N_ACT_REGROUP = (1, 1, 1, 1)
+FLOPS = 4 * 2 * NTOK * C * C
 
 V_W, V_U, V_MUR, V_MUK, V_MUV, V_A0, V_B0 = 0, 1, 2, 3, 4, 5, 9
 
@@ -37,8 +35,6 @@ def tile_rwkv_timemix_pa_kernel(
         keep = ctx.enter_context(tc.tile_pool(name="keep", bufs=1))
         gpool = ctx.enter_context(tc.tile_pool(name="gpool", bufs=2))
         psum = ctx.enter_context(tc.psum_pool(name="psum", bufs=8))
-        if PIN:
-            ctx.enter_context(tc.manual_schedule())
 
         def bank_tile(name):
             return psum.tile([P, HALF], F32, tag="ps", name=name)
@@ -78,31 +74,30 @@ def tile_rwkv_timemix_pa_kernel(
         q = keep.tile([P, 8, NTOK], F32)
         gam = {}
 
-        def gamma(grp, part, parts):
-            h, g2 = grp // 2, grp % 2
+        def sigmoid_table(grp, part):
+            h, g = grp // 2, grp % 2
             if part == 0:
                 gam[grp] = gpool.tile([P, 4, HALF], F32, tag="gam", name="gam")
-            todo = [(j, bb) for j in range(4) for bb in range(2)]
-            n = len(todo) // parts
-            for j, bb in todo[part * n : part * n + n]:
-                m, b = 4 * g2 + j, 2 * h + bb
-                nc.scalar.activation(
-                    out=gam[grp][:, j, T * bb : T * bb + T],
-                    in_=iota1[:],
-                    func=AF.Sigmoid,
-                    scale=negw[:, m : m + 1],
-                    bias=gbias[:, 8 * b + m : 8 * b + m + 1],
-                )
+            for j in (2 * part, 2 * part + 1):
+                for bb in range(2):
+                    m, b = 4 * g + j, 2 * h + bb
+                    nc.scalar.activation(
+                        out=gam[grp][:, j, T * bb : T * bb + T],
+                        in_=iota1[:],
+                        func=AF.Sigmoid,
+                        scale=negw[:, m : m + 1],
+                        bias=gbias[:, 8 * b + m : 8 * b + m + 1],
+                    )
 
-        wnat, wgt, cur = {}, {}, {}
+        wnat, wgt = {}, {}
 
-        def w_load(s):
+        def w_load(pool, s):
             wi, t4 = s // 4, s % 4
             if wi < 3:
-                view = weights[wi].rearrange("(g r e) c -> r g e c", r=P, e=2)
+                view = weights[wi].rearrange("(t r e) c -> r t e c", r=P, e=2)
             else:
-                view = weights[wi].rearrange("(g e r) c -> r g e c", r=P, e=2)
-            wn = cur["pool"].tile([P, 2, C], BF16, tag="wnat", bufs=3, name="wnat")
+                view = weights[wi].rearrange("(t e r) c -> r t e c", r=P, e=2)
+            wn = pool.tile([P, 2, C], BF16, tag="wnat", bufs=3, name="wnat")
             nc.sync.dma_start(out=wn[:, :, :], in_=view[:, t4, :, :])
             wnat[s] = wn
 
@@ -118,9 +113,9 @@ def tile_rwkv_timemix_pa_kernel(
                     )
             return bank
 
-        def w_evac(s, g, bank):
+        def w_evac(pool, s, g, bank):
             if g == 0:
-                wgt[s] = cur["pool"].tile([P, 2, HALF], F32, tag="wg", bufs=2, align_bytes=64, name="wg")
+                wgt[s] = pool.tile([P, 2, HALF], F32, tag="wg", bufs=2, align_bytes=64, name="wg")
             nc.scalar.copy(
                 out=wgt[s][:, g, :].rearrange("p (o u) -> p o u", u=2),
                 in_=bank[:].rearrange("p (u o) -> p o u", u=2),
@@ -135,15 +130,14 @@ def tile_rwkv_timemix_pa_kernel(
                         scales=wos[:, g, T * t4 : T * t4 + T],
                         in_=wgt[s][:, g, :].bitcast(BF16),
                     )
-                return
-            nc.vector.quantize_mx(
-                out=wc[wi][:, t4, :, :].rearrange("p g o -> p (g o)").bitcast(FP8X4),
-                scales=ws[wi][:, t4, :, :].rearrange("p g o -> p (g o)"),
-                in_=wgt[s][:].rearrange("p g w -> p (g w)").bitcast(BF16),
-            )
+            else:
+                nc.vector.quantize_mx(
+                    out=wc[wi][:, t4, :, :].rearrange("p g o -> p (g o)").bitcast(FP8X4),
+                    scales=ws[wi][:, t4, :, :].rearrange("p g o -> p (g o)"),
+                    in_=wgt[s][:].rearrange("p g w -> p (g w)").bitcast(BF16),
+                )
 
-        def phase_a(pa):
-            cur["pool"] = pa
+        def mixes_and_weights(pa):
             xs_nat, x_nat, xsT, dbank, planes = {}, {}, {}, {}, {}
 
             def load_x(h, pieces):
@@ -166,7 +160,7 @@ def tile_rwkv_timemix_pa_kernel(
                             in_=x_prev0[2 * h : 2 * h + 2, :].rearrange("(o b) c -> o b c", o=1),
                         )
 
-            def xs_block(h, gu, on_act):
+            def shifted_block(h, gu):
                 bank = bank_tile("ps_xs")
                 for i in range(4):
                     nc.tensor.transpose(
@@ -175,13 +169,13 @@ def tile_rwkv_timemix_pa_kernel(
                         identF[:],
                     )
                 t = pa.tile([P, HALF], F32, tag="xsT", bufs=5, name="xsT")
-                if on_act:
+                if h == 1:
                     nc.scalar.copy(out=t[:], in_=bank[:])
                 else:
                     nc.vector.tensor_copy(out=t[:], in_=bank[:])
                 xsT[(h, gu)] = t
 
-            def d_plane(s):
+            def difference_plane(s):
                 h, m = s // 8, s % 8
                 gu, e = m // 2, m % 2
                 bank = bank_tile("ps_d")
@@ -215,17 +209,14 @@ def tile_rwkv_timemix_pa_kernel(
                         op1=ALU.add,
                     )
 
-            def regroup(grp, mix, on_act):
+            def regroup(grp, mix):
                 grouped = pa.tile([P, HALF, 4], BF16, tag="grouped", bufs=3, align_bytes=64, name="grouped")
                 dst = grouped[:].rearrange("p (c i) j -> p c j i", i=4)
                 src = planes[grp][mix][:].rearrange("p j (c i) -> p c j i", i=4)
-                if on_act:
-                    nc.scalar.copy(out=dst, in_=src)
-                else:
-                    nc.vector.tensor_copy(out=dst, in_=src)
+                nc.vector.tensor_copy(out=dst, in_=src)
                 return (grp, mix, grouped)
 
-            def x_quant(item):
+            def quantise_mix(item):
                 grp, mix, grouped = item
                 h, g = grp // 2, grp % 2
                 tok = slice(HALF * h, HALF * h + HALF)
@@ -248,7 +239,7 @@ def tile_rwkv_timemix_pa_kernel(
             nc.scalar.dma_start(out=sm[4 * V_B0 : 4 * V_B0 + 16, :], in_=b0.rearrange("b (r c) -> (b r) c", c=256))
             load_x(0, 2)
             for s in range(3):
-                w_load(s)
+                w_load(pa, s)
             load_x(1, 1)
 
             ps_sm = bank_tile("ps_sm")
@@ -261,63 +252,48 @@ def tile_rwkv_timemix_pa_kernel(
                 nc.scalar.activation(out=dec[:, m, :], in_=iota1[:], func=AF.Exp, scale=negw[:, m : m + 1])
             nc.scalar.activation(out=gbias[:], in_=sc[:, 8 * V_B0 : 8 * V_B0 + 32], func=AF.Ln)
             for gu in range(4):
-                xs_block(0, gu, False)
-            d_plane(0)
-            d_plane(1)
+                shifted_block(0, gu)
+            difference_plane(0)
+            difference_plane(1)
             nc.vector.reciprocal(out=rb[:], in_=sc[:, 8 * V_B0 : 8 * V_B0 + 32])
             nc.vector.tensor_tensor(out=alpha[:], in0=sc[:, 8 * V_A0 : 8 * V_A0 + 32], in1=rb[:], op=ALU.mult)
             nc.vector.tensor_scalar_add(out=gbias[:], in0=gbias[:], scalar1=-math.log(EPS))
 
-            act_regroups = []
-            quants = {}
-            n_ln = 0
+            to_quantise = {}
             for s in range(16):
                 if s + 2 < 16:
-                    d_plane(s + 2)
+                    difference_plane(s + 2)
                 banks = [w_transposes(s, g) for g in range(2)] if s < 12 else []
                 if s + 3 < 12:
-                    w_load(s + 3)
+                    w_load(pa, s + 3)
                 if 3 <= s < 7:
-                    xs_block(1, s - 3, True)
+                    shifted_block(1, s - 3)
                 for g in range(len(banks)):
-                    w_evac(s, g, banks[g])
-                for k in range(3):
-                    if n_ln < 32:
-                        ln_table(n_ln)
-                        n_ln += 1
-                if act_regroups:
-                    grp, mix = act_regroups[0]
-                    act_regroups = act_regroups[1:]
-                    quants[s + 1] = quants.get(s + 1, []) + [regroup(grp, mix, True)]
+                    w_evac(pa, s, g, banks[g])
+                for n in range(3 * s, min(3 * s + 3, 32)):
+                    ln_table(n)
                 if s >= 12:
-                    gamma((s - 12) // 2, s % 2, 2)
+                    sigmoid_table((s - 12) // 2, s % 2)
                 mix_plane(s)
                 if 0 < s < 13:
                     w_quant(s - 1)
-                for item in quants.get(s, []):
-                    x_quant(item)
+                for item in to_quantise.get(s, []):
+                    quantise_mix(item)
                 if s % 4 == 3:
-                    grp = s // 4
-                    n_act = N_ACT_REGROUP[grp]
-                    act_regroups = [(grp, mix) for mix in range(n_act)]
-                    for mix in range(n_act, 3):
-                        quants[s + 1] = quants.get(s + 1, []) + [regroup(grp, mix, False)]
-            for grp, mix in act_regroups:
-                quants[16] = quants.get(16, []) + [regroup(grp, mix, True)]
-            for item in quants.get(16, []):
-                x_quant(item)
+                    to_quantise[s + 1] = [regroup(s // 4, mix) for mix in range(3)]
+            for item in to_quantise[16]:
+                quantise_mix(item)
 
-        def phase_b(pb):
-            cur["pool"] = pb
+        def stages(pb):
             acc, ygrp, wgrp, rgrp, ots, held = {}, {}, {}, {}, {}, {}
 
             def flat(t):
                 return t[:].rearrange("p j t -> p (j t)")
 
-            def runs(t, cols):
+            def runs_of_four(t, cols):
                 return t[:, :, cols].rearrange("p j (c i) -> p c j i", i=4)
 
-            def mx1(un):
+            def stage1_matmuls(un):
                 h, m = un // 8, un % 8
                 tok = slice(HALF * h, HALF * h + HALF)
                 mc = slice(P * (m % 2), P * (m % 2) + P)
@@ -335,7 +311,7 @@ def tile_rwkv_timemix_pa_kernel(
                         )
                     acc[(un, wi)] = ps
 
-            def front(un):
+            def out_of_psum(un):
                 h, m = un // 8, un % 8
                 j, grp = un % 4, un // 4
                 tok = slice(HALF * h, HALF * h + HALF)
@@ -359,14 +335,34 @@ def tile_rwkv_timemix_pa_kernel(
                         op1=ALU.subtract,
                     )
 
-            def long_step(grp, k):
-                h, g2 = grp // 2, grp % 2
+            def gate(grp, lo, hi):
+                cols = slice(lo, hi)
+                grouped = pb.tile([P, hi - lo, 4], BF16, tag="grouped", bufs=2, align_bytes=64, name="grouped")
+                nc.vector.tensor_tensor(
+                    out=grouped[:].rearrange("p (c i) j -> p c j i", i=4),
+                    in0=runs_of_four(wgrp[grp], cols),
+                    in1=runs_of_four(rgrp[grp], cols),
+                    op=ALU.mult,
+                )
+                return grouped
+
+            def quantise_h(grp, lo, hi, grouped):
+                h, g = grp // 2, grp % 2
+                tok = slice(HALF * h + lo, HALF * h + hi)
+                nc.vector.quantize_mx(
+                    out=hc[:, g, tok].bitcast(FP8X4),
+                    scales=hs[:, g, tok],
+                    in_=grouped[:].rearrange("p t j -> p (t j)"),
+                )
+
+            def group_step(grp, k):
+                h, g = grp // 2, grp % 2
                 if k == 0:
                     nc.vector.tensor_tensor(out=flat(wgrp[grp]), in0=flat(wgrp[grp]), in1=flat(ygrp[grp]), op=ALU.mult)
                 elif k == 1:
                     for j in range(4):
                         for bb in range(2):
-                            m, b = 4 * g2 + j, 2 * h + bb
+                            m, b = 4 * g + j, 2 * h + bb
                             cols = slice(T * bb, T * bb + T)
                             nc.vector.scalar_tensor_tensor(
                                 out=wgrp[grp][:, j, cols],
@@ -377,21 +373,9 @@ def tile_rwkv_timemix_pa_kernel(
                                 op1=ALU.subtract,
                             )
                 elif k == 2:
-                    grouped = pb.tile([P, HALF, 4], BF16, tag="grouped", bufs=2, align_bytes=64, name="grouped")
-                    nc.vector.tensor_tensor(
-                        out=grouped[:].rearrange("p (c i) j -> p c j i", i=4),
-                        in0=runs(wgrp[grp], slice(0, HALF)),
-                        in1=runs(rgrp[grp], slice(0, HALF)),
-                        op=ALU.mult,
-                    )
-                    held[grp] = grouped
+                    held[grp] = gate(grp, 0, HALF)
                 else:
-                    tok = slice(HALF * h, HALF * h + HALF)
-                    nc.vector.quantize_mx(
-                        out=hc[:, g2, tok].bitcast(FP8X4),
-                        scales=hs[:, g2, tok],
-                        in_=held[grp][:].rearrange("p t j -> p (t j)"),
-                    )
+                    quantise_h(grp, 0, HALF, held[grp])
 
             def stage2_pass(h, n, g, ps):
                 tt, oh = n // 2, n % 2
@@ -406,13 +390,13 @@ def tile_rwkv_timemix_pa_kernel(
                     stop=(g == 1),
                 )
 
-            def stage2_out(h, n, ps, on_act):
+            def stage2_out(h, n, ps, on_scalar):
                 tt, oh = n // 2, n % 2
                 t0 = HALF * h + P * tt
                 if n % 4 == 0:
                     ots[h] = pb.tile([P, 2, C], F32, tag="ot", bufs=2, name="ot")
                 dst = ots[h][:, tt % 2, HALF * oh : HALF * oh + HALF]
-                if on_act:
+                if on_scalar:
                     nc.scalar.copy(out=dst, in_=ps[:])
                 else:
                     nc.vector.tensor_copy(out=dst, in_=ps[:])
@@ -420,30 +404,30 @@ def tile_rwkv_timemix_pa_kernel(
                     nc.sync.dma_start(out=out_flat[t0 : t0 + P, :], in_=ots[h][:, tt % 2, :])
 
             for s in range(12, 15):
-                w_load(s)
+                w_load(pb, s)
             for un in range(4):
-                mx1(un)
-                front(un)
+                stage1_matmuls(un)
+                out_of_psum(un)
             open_banks = []
             for grp in range(4):
                 for k in range(4):
                     if grp < 3:
-                        mx1(4 * grp + 4 + k)
-                        front(4 * grp + 4 + k)
+                        stage1_matmuls(4 * grp + 4 + k)
+                        out_of_psum(4 * grp + 4 + k)
                     if grp < 3 or k < 2:
-                        long_step(grp, k)
+                        group_step(grp, k)
                     if grp == 0:
                         banks = [w_transposes(12 + k, g) for g in range(2)]
                         if k == 0:
-                            w_load(15)
+                            w_load(pb, 15)
                         for g in range(2):
-                            w_evac(12 + k, g, banks[g])
+                            w_evac(pb, 12 + k, g, banks[g])
                         if k > 0:
                             w_quant(11 + k)
                     if grp == 1 and k == 0:
                         w_quant(15)
                     if grp < 2 and k >= 2:
-                        gamma(grp + 2, k - 2, 2)
+                        sigmoid_table(grp + 2, k - 2)
                     if grp == 2:
                         for n in (2 * k, 2 * k + 1):
                             ps = bank_tile("ps_s2")
@@ -454,29 +438,15 @@ def tile_rwkv_timemix_pa_kernel(
                         for n in range(8):
                             open_banks.append(bank_tile("ps_s2"))
                             stage2_pass(1, n, 0, open_banks[n])
-            last = []
-            for part in range(2):
-                cols = slice(T * part, T * part + T)
-                grouped = pb.tile([P, T, 4], BF16, tag="grouped", bufs=2, align_bytes=64, name="grouped")
-                nc.vector.tensor_tensor(
-                    out=grouped[:].rearrange("p (c i) j -> p c j i", i=4),
-                    in0=runs(wgrp[3], cols),
-                    in1=runs(rgrp[3], cols),
-                    op=ALU.mult,
-                )
-                last.append(grouped)
-            for part in range(2):
-                tok = slice(HALF + T * part, HALF + T * part + T)
-                nc.vector.quantize_mx(
-                    out=hc[:, 1, tok].bitcast(FP8X4),
-                    scales=hs[:, 1, tok],
-                    in_=last[part][:].rearrange("p t j -> p (t j)"),
-                )
+            parts = ((0, T), (T, HALF))
+            last = [gate(3, lo, hi) for lo, hi in parts]
+            for (lo, hi), grouped in zip(parts, last):
+                quantise_h(3, lo, hi, grouped)
             for n in range(8):
                 stage2_pass(1, n, 1, open_banks[n])
                 stage2_out(1, n, open_banks[n], n % 2 == 0)
 
         with tc.tile_pool(name="pa", bufs=2) as pool_a:
-            phase_a(pool_a)
+            mixes_and_weights(pool_a)
         with tc.tile_pool(name="pb", bufs=2) as pool_b:
-            phase_b(pool_b)
+            stages(pool_b)

@@ -21,6 +21,8 @@ HALF = 512
 EPS = 1e-8
 FLOPS = 4 * 2 * NTOK * C * C
 
+SCALAR_REGROUPS = (2, 2, 2, 1)
+
 V_W, V_U, V_MUR, V_MUK, V_MUV, V_A0, V_B0 = 0, 1, 2, 3, 4, 5, 9
 
 
@@ -213,7 +215,10 @@ def tile_rwkv_timemix_pa_kernel(
                 grouped = pa.tile([P, HALF, 4], BF16, tag="grouped", bufs=3, align_bytes=64, name="grouped")
                 dst = grouped[:].rearrange("p (c i) j -> p c j i", i=4)
                 src = planes[grp][mix][:].rearrange("p j (c i) -> p c j i", i=4)
-                nc.vector.tensor_copy(out=dst, in_=src)
+                if mix < SCALAR_REGROUPS[grp]:
+                    nc.scalar.copy(out=dst, in_=src)
+                else:
+                    nc.vector.tensor_copy(out=dst, in_=src)
                 return (grp, mix, grouped)
 
             def quantise_mix(item):
@@ -272,6 +277,8 @@ def tile_rwkv_timemix_pa_kernel(
                     w_evac(pa, s, g, banks[g])
                 for n in range(3 * s, min(3 * s + 3, 32)):
                     ln_table(n)
+                if s >= 4 and s % 4 < SCALAR_REGROUPS[s // 4 - 1]:
+                    to_quantise[s + 1] = [regroup(s // 4 - 1, s % 4)]
                 if s >= 12:
                     sigmoid_table((s - 12) // 2, s % 2)
                 mix_plane(s)
@@ -280,8 +287,8 @@ def tile_rwkv_timemix_pa_kernel(
                 for item in to_quantise.get(s, []):
                     quantise_mix(item)
                 if s % 4 == 3:
-                    to_quantise[s + 1] = [regroup(s // 4, mix) for mix in range(3)]
-            for item in to_quantise[16]:
+                    to_quantise[s + 1] = [regroup(s // 4, mix) for mix in range(SCALAR_REGROUPS[s // 4], 3)]
+            for item in to_quantise[16] + [regroup(3, mix) for mix in range(SCALAR_REGROUPS[3])]:
                 quantise_mix(item)
 
         def stages(pb):

import math
from contextlib import ExitStack

import concourse.mybir as mybir
from concourse.masks import make_identity

F32 = mybir.dt.float32
BF16 = mybir.dt.bfloat16
U32 = mybir.dt.uint32
U8 = mybir.dt.uint8
I32 = mybir.dt.int32
FP8X4 = mybir.dt.float8_e4m3fn_x4
ALU = mybir.AluOpType
AF = mybir.ActivationFunctionType

P = 128
C = 1024
NTOK = 1024
T = 256
HALF = 512
EPS = 1e-8
FLOPS = 4 * 2 * NTOK * C * C

SCALAR_REGROUPS = (2, 2, 2, 1)

V_W, V_U, V_MUR, V_MUK, V_MUV, V_A0, V_B0 = 0, 1, 2, 3, 4, 5, 9


def tile_rwkv_timemix_pa_kernel(
    tc, x, a0, b0, x_prev0, w, u, mu_r, mu_k, mu_v, W_r, W_k, W_v, W_out, out
):
    nc = tc.nc
    x_flat = x.flatten_outer_dims()
    out_flat = out.flatten_outer_dims()
    weights = (W_r, W_k, W_v, W_out)
    with ExitStack() as ctx:
        keep = ctx.enter_context(tc.tile_pool(name="keep", bufs=1))
        gpool = ctx.enter_context(tc.tile_pool(name="gpool", bufs=2))
        psum = ctx.enter_context(tc.psum_pool(name="psum", bufs=8))

        def bank_tile(name):
            return psum.tile([P, HALF], F32, tag="ps", name=name)

        sm = keep.tile([P, 256], BF16)
        nc.vector.memset(sm[:], 0.0)
        epsT = keep.tile([P, 1], F32)
        nc.vector.memset(epsT[:], EPS)
        identF = keep.tile([P, P], F32)
        make_identity(nc, identF[:])
        identB = keep.tile([P, P], BF16)
        make_identity(nc, identB[:])
        negB = keep.tile([P, P], BF16)
        nc.vector.tensor_scalar_mul(out=negB[:], in0=identB[:], scalar1=-1.0)
        iota_i = keep.tile([P, T], I32)
        nc.gpsimd.iota(iota_i[:], pattern=[[1, T]], base=1, channel_multiplier=0)
        iota1 = keep.tile([P, T], F32)
        nc.vector.tensor_copy(out=iota1[:], in_=iota_i[:])
        smt = keep.tile([P, P], F32)
        sc = keep.tile([P, 256], F32)
        negw = keep.tile([P, 8], F32)
        rb = keep.tile([P, 32], F32)
        alpha = keep.tile([P, 32], F32)
        gbias = keep.tile([P, 32], F32)

        def scal(v, m):
            return sc[:, 8 * v + m : 8 * v + m + 1]

        wc = [keep.tile([P, 4, 2, T], U32, align_bytes=64, name="wc%d" % i) for i in range(3)]
        ws = [keep.tile([P, 4, 2, T], U8, align_bytes=64, name="ws%d" % i) for i in range(3)]
        woc = keep.tile([P, 2, C], U32, align_bytes=64)
        wos = keep.tile([P, 2, C], U8, align_bytes=64)
        xc = [keep.tile([P, 2, NTOK], U32, align_bytes=64, name="xc%d" % i) for i in range(3)]
        xsc = [keep.tile([P, 2, NTOK], U8, align_bytes=64, name="xsc%d" % i) for i in range(3)]
        hc = keep.tile([P, 2, NTOK], U32, align_bytes=64)
        hs = keep.tile([P, 2, NTOK], U8, align_bytes=64)
        q = keep.tile([P, 8, NTOK], F32)
        gam = {}

        def sigmoid_table(grp, part):
            h, g = grp // 2, grp % 2
            if part == 0:
                gam[grp] = gpool.tile([P, 4, HALF], F32, tag="gam", name="gam")
            for j in (2 * part, 2 * part + 1):
                for bb in range(2):
                    m, b = 4 * g + j, 2 * h + bb
                    nc.scalar.activation(
                        out=gam[grp][:, j, T * bb : T * bb + T],
                        in_=iota1[:],
                        func=AF.Sigmoid,
                        scale=negw[:, m : m + 1],
                        bias=gbias[:, 8 * b + m : 8 * b + m + 1],
                    )

        wnat, wgt = {}, {}

        def w_load(pool, s):
            wi, t4 = s // 4, s % 4
            if wi < 3:
                view = weights[wi].rearrange("(t r e) c -> r t e c", r=P, e=2)
            else:
                view = weights[wi].rearrange("(t e r) c -> r t e c", r=P, e=2)
            wn = pool.tile([P, 2, C], BF16, tag="wnat", bufs=3, name="wnat")
            nc.sync.dma_start(out=wn[:, :, :], in_=view[:, t4, :, :])
            wnat[s] = wn

        def w_transposes(s, g):
            bank = bank_tile("ps_w")
            for uu in range(2):
                for blk in range(2):
                    col = (2 * uu + blk) * P
                    nc.tensor.transpose(
                        bank[:, col : col + P],
                        wnat[s][:, blk, :].bitcast(F32)[:, 256 * g + P * uu : 256 * g + P * uu + P],
                        identF[:],
                    )
            return bank

        def w_evac(pool, s, g, bank):
            if g == 0:
                wgt[s] = pool.tile([P, 2, HALF], F32, tag="wg", bufs=2, align_bytes=64, name="wg")
            nc.scalar.copy(
                out=wgt[s][:, g, :].rearrange("p (o u) -> p o u", u=2),
                in_=bank[:].rearrange("p (u o) -> p o u", u=2),
            )

        def w_quant(s):
            wi, t4 = s // 4, s % 4
            if wi == 3:
                for g in range(2):
                    nc.vector.quantize_mx(
                        out=woc[:, g, T * t4 : T * t4 + T].bitcast(FP8X4),
                        scales=wos[:, g, T * t4 : T * t4 + T],
                        in_=wgt[s][:, g, :].bitcast(BF16),
                    )
            else:
                nc.vector.quantize_mx(
                    out=wc[wi][:, t4, :, :].rearrange("p g o -> p (g o)").bitcast(FP8X4),
                    scales=ws[wi][:, t4, :, :].rearrange("p g o -> p (g o)"),
                    in_=wgt[s][:].rearrange("p g w -> p (g w)").bitcast(BF16),
                )

        def mixes_and_weights(pa):
            xs_nat, x_nat, xsT, dbank, planes = {}, {}, {}, {}, {}

            def load_x(h, pieces):
                xs_t = pa.tile([P, 4, C], BF16, tag="xnat", bufs=4, name="xs_nat")
                x_t = pa.tile([P, 4, C], BF16, tag="xnat", bufs=4, name="x_nat")
                xs_nat[h] = xs_t
                x_nat[h] = x_t
                rows = x_flat[HALF * h : HALF * h + HALF, :]
                by_batch = rows.rearrange("(k p) c -> p k c", p=T)
                width = C // pieces
                for n in range(pieces):
                    cs = slice(width * n, width * n + width)
                    nc.sync.dma_start(out=xs_t[8:128, 0:4:2, cs], in_=by_batch[7:127, :, cs])
                    nc.sync.dma_start(out=xs_t[:, 1:4:2, cs], in_=by_batch[127:255, :, cs])
                    nc.sync.dma_start(out=x_t[:, :, cs], in_=rows[:, cs].rearrange("(i p) c -> p i c", p=P))
                    if n == 0:
                        nc.sync.dma_start(out=xs_t[1:8, 0:4:2, :], in_=by_batch[0:7, :, :])
                        nc.sync.dma_start(
                            out=xs_t[0:1, 0:4:2, :],
                            in_=x_prev0[2 * h : 2 * h + 2, :].rearrange("(o b) c -> o b c", o=1),
                        )

            def shifted_block(h, gu):
                bank = bank_tile("ps_xs")
                for i in range(4):
                    nc.tensor.transpose(
                        bank[:, P * i : P * i + P],
                        xs_nat[h][:, i, :].bitcast(F32)[:, P * gu : P * gu + P],
                        identF[:],
                    )
                t = pa.tile([P, HALF], F32, tag="xsT", bufs=5, name="xsT")
                if h == 1:
                    nc.scalar.copy(out=t[:], in_=bank[:])
                else:
                    nc.vector.tensor_copy(out=t[:], in_=bank[:])
                xsT[(h, gu)] = t

            def difference_plane(s):
                h, m = s // 8, s % 8
                gu, e = m // 2, m % 2
                bank = bank_tile("ps_d")
                lo, hi = 256 * gu + e, 256 * gu + 256
                for i in range(4):
                    nc.tensor.matmul(
                        bank[:, P * i : P * i + P], lhsT=x_nat[h][:, i, lo:hi:2], rhs=identB[:],
                        start=True, stop=False,
                    )
                    nc.tensor.matmul(
                        bank[:, P * i : P * i + P], lhsT=xs_nat[h][:, i, lo:hi:2], rhs=negB[:],
                        start=False, stop=True,
                    )
                dbank[s] = bank

            def mix_plane(s):
                h, m = s // 8, s % 8
                gu, e, j, grp = m // 2, m % 2, m % 4, s // 4
                if j == 0:
                    planes[grp] = [
                        pa.tile([P, 4, HALF], BF16, tag="planes", bufs=6, name="planes%d" % i) for i in range(3)
                    ]
                shifted = xsT[(h, gu)][:].bitcast(BF16).rearrange("p (t e) -> p t e", e=2)[:, :, e]
                for mix in range(3):
                    nc.vector.scalar_tensor_tensor(
                        out=planes[grp][mix][:, j, :],
                        in0=dbank[s][:],
                        scalar=scal(V_MUR + mix, m),
                        in1=shifted,
                        op0=ALU.mult,
                        op1=ALU.add,
                    )

            def regroup(grp, mix):
                grouped = pa.tile([P, HALF, 4], BF16, tag="grouped", bufs=3, align_bytes=64, name="grouped")
                dst = grouped[:].rearrange("p (c i) j -> p c j i", i=4)
                src = planes[grp][mix][:].rearrange("p j (c i) -> p c j i", i=4)
                if mix < SCALAR_REGROUPS[grp]:
                    nc.scalar.copy(out=dst, in_=src)
                else:
                    nc.vector.tensor_copy(out=dst, in_=src)
                return (grp, mix, grouped)

            def quantise_mix(item):
                grp, mix, grouped = item
                h, g = grp // 2, grp % 2
                tok = slice(HALF * h, HALF * h + HALF)
                nc.vector.quantize_mx(
                    out=xc[mix][:, g, tok].bitcast(FP8X4),
                    scales=xsc[mix][:, g, tok],
                    in_=grouped[:].rearrange("p t j -> p (t j)"),
                )

            def ln_table(n):
                m, b = n // 4, n % 4
                nc.scalar.activation(
                    out=q[:, m, T * b : T * b + T], in_=dec[:, m, :], func=AF.Ln,
                    scale=scal(V_B0 + b, m), bias=epsT[:],
                )

            for v, vec in ((V_W, w), (V_U, u), (V_MUR, mu_r), (V_MUK, mu_k), (V_MUV, mu_v)):
                nc.scalar.dma_start(out=sm[4 * v : 4 * v + 4, :], in_=vec.rearrange("(r c) -> r c", c=256))
            nc.scalar.dma_start(out=sm[4 * V_A0 : 4 * V_A0 + 16, :], in_=a0.rearrange("b (r c) -> (b r) c", c=256))
            nc.scalar.dma_start(out=sm[4 * V_B0 : 4 * V_B0 + 16, :], in_=b0.rearrange("b (r c) -> (b r) c", c=256))
            load_x(0, 2)
            for s in range(3):
                w_load(pa, s)
            load_x(1, 1)

            ps_sm = bank_tile("ps_sm")
            nc.tensor.transpose(ps_sm[:, 0:P], sm[:].bitcast(F32), identF[:])
            nc.vector.tensor_copy(out=smt[:], in_=ps_sm[:, 0:P])
            nc.vector.tensor_copy(out=sc[:], in_=smt[:].bitcast(BF16))
            nc.vector.tensor_scalar_mul(out=negw[:], in0=sc[:, 8 * V_W : 8 * V_W + 8], scalar1=-1.0)
            dec = gpool.tile([P, 8, T], F32, tag="gam", name="dec")
            for m in range(8):
                nc.scalar.activation(out=dec[:, m, :], in_=iota1[:], func=AF.Exp, scale=negw[:, m : m + 1])
            nc.scalar.activation(out=gbias[:], in_=sc[:, 8 * V_B0 : 8 * V_B0 + 32], func=AF.Ln)
            for gu in range(4):
                shifted_block(0, gu)
            difference_plane(0)
            difference_plane(1)
            nc.vector.reciprocal(out=rb[:], in_=sc[:, 8 * V_B0 : 8 * V_B0 + 32])
            nc.vector.tensor_tensor(out=alpha[:], in0=sc[:, 8 * V_A0 : 8 * V_A0 + 32], in1=rb[:], op=ALU.mult)
            nc.vector.tensor_scalar_add(out=gbias[:], in0=gbias[:], scalar1=-math.log(EPS))

            to_quantise = {}
            for s in range(16):
                if s + 2 < 16:
                    difference_plane(s + 2)
                banks = [w_transposes(s, g) for g in range(2)] if s < 12 else []
                if s + 3 < 12:
                    w_load(pa, s + 3)
                if 3 <= s < 7:
                    shifted_block(1, s - 3)
                for g in range(len(banks)):
                    w_evac(pa, s, g, banks[g])
                for n in range(3 * s, min(3 * s + 3, 32)):
                    ln_table(n)
                if s >= 4 and s % 4 < SCALAR_REGROUPS[s // 4 - 1]:
                    to_quantise[s + 1] = [regroup(s // 4 - 1, s % 4)]
                if s >= 12:
                    sigmoid_table((s - 12) // 2, s % 2)
                mix_plane(s)
                if 0 < s < 13:
                    w_quant(s - 1)
                for item in to_quantise.get(s, []):
                    quantise_mix(item)
                if s % 4 == 3:
                    to_quantise[s + 1] = [regroup(s // 4, mix) for mix in range(SCALAR_REGROUPS[s // 4], 3)]
            for item in to_quantise[16] + [regroup(3, mix) for mix in range(SCALAR_REGROUPS[3])]:
                quantise_mix(item)

        def stages(pb):
            acc, ygrp, wgrp, rgrp, ots, held = {}, {}, {}, {}, {}, {}

            def flat(t):
                return t[:].rearrange("p j t -> p (j t)")

            def runs_of_four(t, cols):
                return t[:, :, cols].rearrange("p j (c i) -> p c j i", i=4)

            def stage1_matmuls(un):
                h, m = un // 8, un % 8
                tok = slice(HALF * h, HALF * h + HALF)
                mc = slice(P * (m % 2), P * (m % 2) + P)
                for wi in (1, 2, 0):
                    ps = bank_tile("ps_s1")
                    for g in range(2):
                        nc.tensor.matmul_mx(
                            out=ps[:],
                            lhsT=wc[wi][:, m // 2, g, mc].bitcast(FP8X4),
                            lhsT_scale=ws[wi][:, m // 2, g, mc],
                            rhs=xc[wi][:, g, tok].bitcast(FP8X4),
                            rhs_scale=xsc[wi][:, g, tok],
                            start=(g == 0),
                            stop=(g == 1),
                        )
                    acc[(un, wi)] = ps

            def out_of_psum(un):
                h, m = un // 8, un % 8
                j, grp = un % 4, un // 4
                tok = slice(HALF * h, HALF * h + HALF)
                if j == 0:
                    ygrp[grp] = pb.tile([P, 4, HALF], F32, tag="grp", bufs=6, name="ygrp")
                    wgrp[grp] = pb.tile([P, 4, HALF], F32, tag="grp", bufs=6, name="wgrp")
                    rgrp[grp] = pb.tile([P, 4, HALF], F32, tag="grp", bufs=6, name="rgrp")
                y_t = ygrp[grp][:, j, :]
                nc.vector.tensor_tensor(out=y_t, in0=acc[(un, 1)][:], in1=q[:, m, tok], op=ALU.subtract)
                nc.scalar.activation(out=y_t, in_=y_t, func=AF.Sigmoid, bias=scal(V_U, m))
                nc.scalar.activation(out=rgrp[grp][:, j, :], in_=acc[(un, 0)][:], func=AF.Sigmoid)
                for bb in range(2):
                    b = 2 * h + bb
                    cols = slice(T * bb, T * bb + T)
                    nc.vector.scalar_tensor_tensor(
                        out=wgrp[grp][:, j, cols],
                        in0=gam[grp][:, j, cols],
                        scalar=alpha[:, 8 * b + m : 8 * b + m + 1],
                        in1=acc[(un, 2)][:, cols],
                        op0=ALU.mult,
                        op1=ALU.subtract,
                    )

            def gate(grp, lo, hi):
                cols = slice(lo, hi)
                grouped = pb.tile([P, hi - lo, 4], BF16, tag="grouped", bufs=2, align_bytes=64, name="grouped")
                nc.vector.tensor_tensor(
                    out=grouped[:].rearrange("p (c i) j -> p c j i", i=4),
                    in0=runs_of_four(wgrp[grp], cols),
                    in1=runs_of_four(rgrp[grp], cols),
                    op=ALU.mult,
                )
                return grouped

            def quantise_h(grp, lo, hi, grouped):
                h, g = grp // 2, grp % 2
                tok = slice(HALF * h + lo, HALF * h + hi)
                nc.vector.quantize_mx(
                    out=hc[:, g, tok].bitcast(FP8X4),
                    scales=hs[:, g, tok],
                    in_=grouped[:].rearrange("p t j -> p (t j)"),
                )

            def group_step(grp, k):
                h, g = grp // 2, grp % 2
                if k == 0:
                    nc.vector.tensor_tensor(out=flat(wgrp[grp]), in0=flat(wgrp[grp]), in1=flat(ygrp[grp]), op=ALU.mult)
                elif k == 1:
                    for j in range(4):
                        for bb in range(2):
                            m, b = 4 * g + j, 2 * h + bb
                            cols = slice(T * bb, T * bb + T)
                            nc.vector.scalar_tensor_tensor(
                                out=wgrp[grp][:, j, cols],
                                in0=gam[grp][:, j, cols],
                                scalar=alpha[:, 8 * b + m : 8 * b + m + 1],
                                in1=wgrp[grp][:, j, cols],
                                op0=ALU.mult,
                                op1=ALU.subtract,
                            )
                elif k == 2:
                    held[grp] = gate(grp, 0, HALF)
                else:
                    quantise_h(grp, 0, HALF, held[grp])

            def stage2_pass(h, n, g, ps):
                tt, oh = n // 2, n % 2
                t0 = HALF * h + P * tt
                nc.tensor.matmul_mx(
                    out=ps[:],
                    lhsT=hc[:, g, t0 : t0 + P].bitcast(FP8X4),
                    lhsT_scale=hs[:, g, t0 : t0 + P],
                    rhs=woc[:, g, HALF * oh : HALF * oh + HALF].bitcast(FP8X4),
                    rhs_scale=wos[:, g, HALF * oh : HALF * oh + HALF],
                    start=(g == 0),
                    stop=(g == 1),
                )

            def stage2_out(h, n, ps, on_scalar):
                tt, oh = n // 2, n % 2
                t0 = HALF * h + P * tt
                if n % 4 == 0:
                    ots[h] = pb.tile([P, 2, C], F32, tag="ot", bufs=2, name="ot")
                dst = ots[h][:, tt % 2, HALF * oh : HALF * oh + HALF]
                if on_scalar:
                    nc.scalar.copy(out=dst, in_=ps[:])
                else:
                    nc.vector.tensor_copy(out=dst, in_=ps[:])
                if oh == 1:
                    nc.sync.dma_start(out=out_flat[t0 : t0 + P, :], in_=ots[h][:, tt % 2, :])

            for s in range(12, 15):
                w_load(pb, s)
            for un in range(4):
                stage1_matmuls(un)
                out_of_psum(un)
            open_banks = []
            for grp in range(4):
                for k in range(4):
                    if grp < 3:
                        stage1_matmuls(4 * grp + 4 + k)
                        out_of_psum(4 * grp + 4 + k)
                    if grp < 3 or k < 2:
                        group_step(grp, k)
                    if grp == 0:
                        banks = [w_transposes(12 + k, g) for g in range(2)]
                        if k == 0:
                            w_load(pb, 15)
                        for g in range(2):
                            w_evac(pb, 12 + k, g, banks[g])
                        if k > 0:
                            w_quant(11 + k)
                    if grp == 1 and k == 0:
                        w_quant(15)
                    if grp < 2 and k >= 2:
                        sigmoid_table(grp + 2, k - 2)
                    if grp == 2:
                        for n in (2 * k, 2 * k + 1):
                            ps = bank_tile("ps_s2")
                            stage2_pass(0, n, 0, ps)
                            stage2_pass(0, n, 1, ps)
                            stage2_out(0, n, ps, True)
                    if grp == 3 and k == 0:
                        for n in range(8):
                            open_banks.append(bank_tile("ps_s2"))
                            stage2_pass(1, n, 0, open_banks[n])
            parts = ((0, T), (T, HALF))
            last = [gate(3, lo, hi) for lo, hi in parts]
            for (lo, hi), grouped in zip(parts, last):
                quantise_h(3, lo, hi, grouped)
            for n in range(8):
                stage2_pass(1, n, 1, open_banks[n])
                stage2_out(1, n, open_banks[n], n % 2 == 0)

        with tc.tile_pool(name="pa", bufs=2) as pool_a:
            mixes_and_weights(pool_a)
        with tc.tile_pool(name="pb", bufs=2) as pool_b:
            stages(pool_b)
